import numpy as np
import ml_dtypes


def mxq(x, axis, fmt="e4m3"):
    dtype, down = {"e4m3": (ml_dtypes.float8_e4m3fn, 7), "e5m2": (ml_dtypes.float8_e5m2, 14)}[fmt]
    v = np.moveaxis(np.asarray(x, np.float32).astype(ml_dtypes.bfloat16).astype(np.float64), axis, -1)
    blocks = v.reshape(v.shape[:-1] + (-1, 32))
    amax = np.abs(blocks).max(-1, keepdims=True)
    byte = np.maximum(np.where(amax > 0, np.frexp(amax)[1] - 1 + 127, 0) - down, 1)
    scale = np.exp2(byte - 127.0)
    codes = (blocks / scale).astype(np.float32).astype(dtype).astype(np.float64)
    return np.moveaxis((codes * scale).reshape(v.shape), -1, axis)


WIDE = False


def mx_kscale(k):
    if not WIDE:
        return np.ones(k)
    levels = np.array([10, -10, 5, -5, 0])
    a = np.random.permutation(np.resize(levels, k // 512 * 4)).reshape(k // 512, 4)
    idx = np.arange(k)
    return np.exp2(a[idx // 512, idx % 128 // 32])


BF16 = ml_dtypes.bfloat16


def bf(x):
    return np.asarray(x, np.float32).astype(BF16)


def f64(x):
    return np.asarray(x).astype(np.float64)


B, H, W, C, D, P = 512, 8, 4, 512, 256, 128
F = H * W * D
STRIDE = 16.0


def safe_exp(v):
    return np.exp(np.clip(v, -10.0, 10.0))


def setup_inputs():
    s = mx_kscale(C)
    t = mx_kscale(F)[:D]
    tf = np.tile(t, H * W)[:, None]
    return {"features": bf(np.random.standard_normal((B, H, W, C)) * s),
            "roi": bf(np.random.uniform(0.02, 0.125, (B, P, 4))),
            "conv_w": bf(np.random.standard_normal((C, D)) / np.sqrt(C) / s[:, None] * t),
            "conv_b": bf(np.random.standard_normal(D) * 0.2 * t),
            "cls_w": bf(np.random.standard_normal((F, 2 * P)) * 1.5 / np.sqrt(F) / tf),
            "cls_b": bf(np.random.standard_normal(2 * P) * 0.5),
            "bbox_w": bf(np.random.standard_normal((F, 4 * P)) * 0.7 / np.sqrt(F) / tf),
            "bbox_b": bf(np.random.standard_normal(4 * P) * 0.3)}


def reference(features, roi, conv_w, conv_b, cls_w, cls_b, bbox_w, bbox_b):
    h = np.maximum((mxq(f64(features).reshape(B * H * W, C), 1, "e4m3") @ mxq(f64(conv_w), 0, "e4m3")) + f64(conv_b), 0.0)
    flatq = mxq(h.reshape(B, F), 1, "e4m3")
    cls = (flatq @ mxq(f64(cls_w), 0, "e4m3")) + f64(cls_b)
    bbox = (flatq @ mxq(f64(bbox_w)[:, P:], 0, "e4m3")) + f64(bbox_b)[P:]
    obj = np.stack([cls[:, :P], cls[:, P:]], axis=0)
    e = np.exp(obj - obj.max(axis=0, keepdims=True))
    objectness = (e / e.sum(axis=0, keepdims=True))[1]
    roi_img = f64(roi) * STRIDE
    bb = np.transpose(bbox.reshape(B, 3, P), (0, 2, 1))
    x = roi_img[:, :, 0] - bb[:, :, 0] * roi_img[:, :, 3]
    y = roi_img[:, :, 1]
    w = roi_img[:, :, 2] * safe_exp(bb[:, :, 1])
    hh = roi_img[:, :, 3] * safe_exp(bb[:, :, 2])
    return np.stack([x, y, w, hh, objectness], axis=-1)

@@ -1,0 +1,334 @@
+from contextlib import ExitStack
+
+import concourse.masks as masks
+import concourse.mybir as mybir
+
+F32 = mybir.dt.float32
+BF16 = mybir.dt.bfloat16
+U32 = mybir.dt.uint32
+U8 = mybir.dt.uint8
+FP8X4 = mybir.dt.float8_e4m3fn_x4
+ACT = mybir.ActivationFunctionType
+ALU = mybir.AluOpType
+
+P = 128
+PACK = 4
+BATCH = 512
+POSITIONS = 32
+CHANNELS = 512
+HIDDEN = 256
+PROPOSALS = 128
+STRIDE = 16.0
+
+CHUNKS = BATCH // P
+STEPS = POSITIONS // PACK
+ROUNDS = STEPS * CHUNKS
+HALVES = HIDDEN // P
+CLS_COLS = 2 * PROPOSALS
+BOX_COLS = 3 * PROPOSALS
+MAIN_COLS = 512
+TAIL_COLS = PROPOSALS
+OUT_COLS = MAIN_COLS + TAIL_COLS
+UNITS_AHEAD = 4
+
+FLOPS = 2 * BATCH * POSITIONS * CHANNELS * HIDDEN + 2 * BATCH * POSITIONS * HIDDEN * OUT_COLS
+BYTES = (
+    2 * (BATCH * POSITIONS * CHANNELS + BATCH * PROPOSALS * 4 + CHANNELS * HIDDEN + HIDDEN)
+    + 2 * (POSITIONS * HIDDEN + 1) * OUT_COLS
+    + 4 * BATCH * PROPOSALS * 5
+)
+
+
+def tile_classifiermodel_t_kernel(
+    tc, features, roi, conv_w, conv_b, cls_w, cls_b, bbox_w, bbox_b, out
+):
+    nc = tc.nc
+    feature_rows = features.rearrange("b i j c -> b (i j) c")
+    cls_rows = cls_w.rearrange("(s p e) n -> p s (e n)", p=P, e=HALVES)
+    box_rows = bbox_w.rearrange("(s p e) n -> p s e n", p=P, e=HALVES)
+
+    with ExitStack() as stack:
+        const = stack.enter_context(tc.tile_pool(name="const", bufs=1))
+        x_pool = stack.enter_context(tc.tile_pool(name="x", bufs=UNITS_AHEAD + 2))
+        raw_pool = stack.enter_context(tc.tile_pool(name="raw", bufs=2))
+        stage = stack.enter_context(tc.tile_pool(name="stage", bufs=3))
+        weights = stack.enter_context(tc.tile_pool(name="weights", bufs=2))
+        finish = stack.enter_context(tc.tile_pool(name="finish", bufs=2))
+        planes_pool = stack.enter_context(tc.tile_pool(name="planes", bufs=CHUNKS))
+        work = stack.enter_context(tc.psum_pool(name="work", bufs=3))
+        sums = stack.enter_context(tc.psum_pool(name="sums", bufs=1))
+
+        x_tiles = {}
+        raw_tiles = {}
+        grouped_weights = {}
+        main_weights = {}
+        x_grouped = {}
+        x_quantised = {}
+        h_grouped = {}
+        roi_tiles = {}
+        planes = {}
+
+        identity = const.tile([P, P], F32)
+        conv_codes = const.tile([P, HIDDEN], U32, align_bytes=64)
+        conv_scales = const.tile([P, HIDDEN], U8, align_bytes=64)
+        conv_bias = const.tile([P, HALVES], F32)
+        out_bias = const.tile([P, OUT_COLS], BF16)
+        h_codes = const.tile([P, STEPS, HALVES, BATCH], U32, align_bytes=64)
+        h_scales = const.tile([P, STEPS, HALVES, BATCH], U8, align_bytes=64)
+        tail_codes = const.tile([P, STEPS, HALVES, TAIL_COLS], U32, align_bytes=64)
+        tail_scales = const.tile([P, STEPS, HALVES, TAIL_COLS], U8, align_bytes=64)
+        main_sums = [sums.tile([P, MAIN_COLS], F32, name="main_sum%d" % m) for m in range(CHUNKS)]
+        tail_sums = sums.tile([P, CHUNKS, TAIL_COLS], F32)
+
+        def load_unit(r):
+            step, m = divmod(r, CHUNKS)
+            x = x_pool.tile([P, PACK, CHANNELS], BF16)
+            nc.sync.dma_start(
+                out=x[:],
+                in_=feature_rows[m * P : (m + 1) * P, step * PACK : (step + 1) * PACK, :],
+            )
+            x_tiles[r] = x
+
+        def load_slab(step):
+            positions = slice(step * PACK, (step + 1) * PACK)
+            cls_raw = raw_pool.tile([P, PACK, HALVES, CLS_COLS], BF16)
+            nc.sync.dma_start(
+                out=cls_raw[:].rearrange("p t e n -> p t (e n)"), in_=cls_rows[:, positions, :]
+            )
+            box_raw = raw_pool.tile([P, PACK, HALVES, BOX_COLS], BF16)
+            for e in range(HALVES):
+                nc.sync.dma_start(
+                    out=box_raw[:, :, e, :], in_=box_rows[:, positions, e, PROPOSALS:]
+                )
+            raw_tiles[step] = (cls_raw, box_raw)
+
+        def regroup_weights(step, piece):
+            e, source = divmod(piece, 2)
+            if piece == 0:
+                w_grouped = weights.tile([P, HALVES, OUT_COLS, PACK], BF16, align_bytes=64)
+                grouped_weights[step] = w_grouped
+            raw = raw_tiles[step][source]
+            first = source * CLS_COLS
+            width = (CLS_COLS, BOX_COLS)[source]
+            nc.vector.tensor_copy(
+                out=grouped_weights[step][:, e, first : first + width, :].rearrange(
+                    "p (c i) t -> p c t i", i=4
+                ),
+                in_=raw[:, :, e, :].rearrange("p t (c i) -> p c t i", i=4),
+            )
+
+        def quantise_weights(step, e):
+            if e == 0:
+                w_codes = weights.tile([P, HALVES, MAIN_COLS], U32, align_bytes=64)
+                w_scales = weights.tile([P, HALVES, MAIN_COLS], U8, align_bytes=64)
+                main_weights[step] = (w_codes, w_scales)
+            w_codes, w_scales = main_weights[step]
+            w_grouped = grouped_weights[step]
+            nc.vector.quantize_mx(
+                out=w_codes[:, e, :].bitcast(FP8X4),
+                scales=w_scales[:, e, :],
+                in_=w_grouped[:, e, :MAIN_COLS, :].rearrange("p n t -> p (n t)"),
+            )
+            nc.vector.quantize_mx(
+                out=tail_codes[:, step, e, :].bitcast(FP8X4),
+                scales=tail_scales[:, step, e, :],
+                in_=w_grouped[:, e, MAIN_COLS:, :].rearrange("p n t -> p (n t)"),
+            )
+
+        def transpose_unit(r):
+            x_words = x_tiles[r][:].bitcast(F32)
+            grouped = stage.tile([P, PACK * P * PACK], BF16, align_bytes=64)
+            grouped_words = grouped[:].bitcast(F32).rearrange("p (r u) -> p r u", u=2)
+            for bank in range(2):
+                turned = work.tile([P, 2, 2 * P], F32, tag="work")
+                for tt in range(2):
+                    for u in range(2):
+                        nc.tensor.transpose(
+                            turned[:, u, tt * P : (tt + 1) * P],
+                            x_words[:, 2 * bank + tt, u * P : (u + 1) * P],
+                            identity[:],
+                        )
+                nc.scalar.copy(
+                    out=grouped_words[:, bank * 2 * P : (bank + 1) * 2 * P, :],
+                    in_=turned[:].rearrange("p u r -> p r u"),
+                )
+            x_grouped[r] = grouped
+
+        def quantise_features(r):
+            x_codes = stage.tile([P, PACK * P], U32, align_bytes=64)
+            x_scales = stage.tile([P, PACK * P], U8, align_bytes=64)
+            nc.vector.quantize_mx(
+                out=x_codes[:].bitcast(FP8X4), scales=x_scales[:], in_=x_grouped[r][:]
+            )
+            x_quantised[r] = (x_codes, x_scales)
+
+        def first_stage(r):
+            x_codes, x_scales = x_quantised[r]
+            hidden = stage.tile([P, HALVES, P, PACK], BF16, align_bytes=64)
+            for e in range(HALVES):
+                h_sum = work.tile([P, PACK * P], F32, tag="work")
+                nc.tensor.matmul_mx(
+                    out=h_sum[:],
+                    lhsT=conv_codes[:, e * P : (e + 1) * P].bitcast(FP8X4),
+                    lhsT_scale=conv_scales[:, e * P : (e + 1) * P],
+                    rhs=x_codes[:].bitcast(FP8X4),
+                    rhs_scale=x_scales[:],
+                    start=True,
+                    stop=True,
+                )
+                nc.scalar.activation(
+                    out=hidden[:, e, :, :],
+                    in_=h_sum[:].rearrange("p (t b) -> p b t", t=PACK),
+                    func=ACT.Relu,
+                    bias=conv_bias[:, e : e + 1],
+                    scale=1.0,
+                )
+            h_grouped[r] = hidden
+
+        def quantise_hidden(r):
+            step, m = divmod(r, CHUNKS)
+            images = slice(m * P, (m + 1) * P)
+            for e in range(HALVES):
+                nc.vector.quantize_mx(
+                    out=h_codes[:, step, e, images].bitcast(FP8X4),
+                    scales=h_scales[:, step, e, images],
+                    in_=h_grouped[r][:, e, :, :].rearrange("p b t -> p (b t)"),
+                )
+
+        def second_stage(r):
+            step, m = divmod(r, CHUNKS)
+            images = slice(m * P, (m + 1) * P)
+            w_codes, w_scales = main_weights[step]
+            for e in range(HALVES):
+                nc.tensor.matmul_mx(
+                    out=main_sums[m][:],
+                    lhsT=h_codes[:, step, e, images].bitcast(FP8X4),
+                    lhsT_scale=h_scales[:, step, e, images],
+                    rhs=w_codes[:, e, :].bitcast(FP8X4),
+                    rhs_scale=w_scales[:, e, :],
+                    start=(step == 0 and e == 0),
+                    stop=(step == STEPS - 1 and e == HALVES - 1),
+                )
+
+        def tail_group(m):
+            images = slice(m * P, (m + 1) * P)
+            for step in range(STEPS):
+                for e in range(HALVES):
+                    nc.tensor.matmul_mx(
+                        out=tail_sums[:, m, :],
+                        lhsT=h_codes[:, step, e, images].bitcast(FP8X4),
+                        lhsT_scale=h_scales[:, step, e, images],
+                        rhs=tail_codes[:, step, e, :].bitcast(FP8X4),
+                        rhs_scale=tail_scales[:, step, e, :],
+                        start=(step == 0 and e == 0),
+                        stop=(step == STEPS - 1 and e == HALVES - 1),
+                    )
+
+        def load_roi(m):
+            roi_raw = planes_pool.tile([P, PROPOSALS * 4], BF16)
+            nc.sync.dma_start(
+                out=roi_raw[:], in_=roi[m * P : (m + 1) * P, :, :].rearrange("b q k -> b (q k)")
+            )
+            roi_tiles[m] = roi_raw
+
+        def scale_roi(m):
+            result = planes_pool.tile([P, 5, PROPOSALS], F32)
+            nc.vector.tensor_scalar_mul(
+                out=result[:, 0:4, :],
+                in0=roi_tiles[m][:].rearrange("p (q k) -> p k q", k=4),
+                scalar1=STRIDE,
+            )
+            planes[m] = result
+
+        def epilogue(m):
+            result = planes[m]
+            z = finish.tile([P, OUT_COLS], F32)
+            nc.vector.tensor_tensor(
+                out=z[:, :MAIN_COLS], in0=main_sums[m][:], in1=out_bias[:, :MAIN_COLS], op=ALU.add
+            )
+            nc.vector.tensor_tensor(
+                out=z[:, MAIN_COLS:], in0=tail_sums[:, m, :], in1=out_bias[:, MAIN_COLS:], op=ALU.add
+            )
+            c0 = z[:, 0:PROPOSALS]
+            c1 = z[:, PROPOSALS : 2 * PROPOSALS]
+            b1 = z[:, 2 * PROPOSALS : 3 * PROPOSALS]
+            b23 = z[:, 3 * PROPOSALS :]
+            logit = finish.tile([P, PROPOSALS], F32)
+            nc.vector.tensor_sub(out=logit[:], in0=c1, in1=c0)
+            nc.vector.tensor_scalar(
+                out=b23, in0=b23, scalar1=-10.0, scalar2=10.0, op0=ALU.max, op1=ALU.min
+            )
+            halfway = finish.tile([P, PROPOSALS], F32)
+            nc.scalar.activation(out=halfway[:], in_=logit[:], func=ACT.Tanh, scale=0.5)
+            growth = finish.tile([P, 2, PROPOSALS], F32)
+            nc.scalar.activation(
+                out=growth[:].rearrange("p j q -> p (j q)"), in_=b23, func=ACT.Exp
+            )
+            shift = finish.tile([P, PROPOSALS], F32)
+            nc.vector.tensor_mul(out=shift[:], in0=b1, in1=result[:, 3, :])
+            nc.vector.tensor_sub(out=result[:, 0, :], in0=result[:, 0, :], in1=shift[:])
+            nc.vector.tensor_scalar(
+                out=result[:, 4, :], in0=halfway[:], scalar1=0.5, scalar2=0.5, op0=ALU.mult, op1=ALU.add
+            )
+            nc.vector.tensor_mul(out=result[:, 2:4, :], in0=result[:, 2:4, :], in1=growth[:])
+            boxes = finish.tile([P, PROPOSALS, 5], F32)
+            nc.scalar.copy(out=boxes[:], in_=result[:].rearrange("p k q -> p q k"))
+            nc.sync.dma_start(out=out[m * P : (m + 1) * P, :, :], in_=boxes[:])
+
+        masks.make_identity(nc, identity[:])
+        conv_raw = const.tile([P, PACK, HIDDEN], BF16)
+        nc.sync.dma_start(
+            out=conv_raw[:].rearrange("p (u e) d -> p u (e d)", e=2),
+            in_=conv_w.rearrange("(u p e) d -> p u (e d)", p=P, e=2),
+        )
+        conv_bias_raw = const.tile([P, HALVES], BF16)
+        nc.sync.dma_start(out=conv_bias_raw[:], in_=conv_b.rearrange("(p e) -> p e", e=HALVES))
+        load_slab(0)
+        for r in range(UNITS_AHEAD):
+            load_unit(r)
+        load_slab(1)
+        nc.sync.dma_start(out=out_bias[:, :CLS_COLS], in_=cls_b.partition_broadcast(P))
+        nc.sync.dma_start(out=out_bias[:, CLS_COLS:], in_=bbox_b[PROPOSALS:].partition_broadcast(P))
+
+        conv_grouped = const.tile([P, HALVES, P, PACK], BF16, align_bytes=64)
+        nc.vector.tensor_copy(
+            out=conv_grouped[:], in_=conv_raw[:].rearrange("p t (j h) -> p h j t", h=HALVES)
+        )
+        nc.vector.tensor_copy(out=conv_bias[:], in_=conv_bias_raw[:])
+        nc.vector.quantize_mx(
+            out=conv_codes[:].bitcast(FP8X4),
+            scales=conv_scales[:],
+            in_=conv_grouped[:].rearrange("p h j t -> p (h j t)"),
+        )
+        for piece in range(4):
+            regroup_weights(0, piece)
+            if piece % 2 == 1:
+                quantise_weights(0, piece // 2)
+
+        for r in range(ROUNDS + 2):
+            step, m = divmod(r, CHUNKS)
+            if r + UNITS_AHEAD < ROUNDS:
+                load_unit(r + UNITS_AHEAD)
+            if m == 0 and step + 2 < STEPS:
+                load_slab(step + 2)
+            if step == STEPS - 2:
+                load_roi(m)
+            if r >= 2:
+                quantise_hidden(r - 2)
+            if r < ROUNDS:
+                transpose_unit(r)
+            if step + 1 < STEPS:
+                regroup_weights(step + 1, m)
+            if step == STEPS - 1:
+                scale_roi(m)
+            if 1 <= r <= ROUNDS:
+                first_stage(r - 1)
+            if r < ROUNDS:
+                quantise_features(r)
+            if r >= 2:
+                second_stage(r - 2)
+            if step + 1 < STEPS and m % 2 == 1:
+                quantise_weights(step + 1, m // 2)
+            if r - 2 >= ROUNDS - CHUNKS:
+                tail_group(r - 2 - (ROUNDS - CHUNKS))
+                epilogue(r - 2 - (ROUNDS - CHUNKS))

@@ -30,6 +30,8 @@ MAIN_COLS = 512
 TAIL_COLS = PROPOSALS
 OUT_COLS = MAIN_COLS + TAIL_COLS
 UNITS_AHEAD = 4
+PIECES = 4
+WEIGHTS_AHEAD = 3
 
 FLOPS = 2 * BATCH * POSITIONS * CHANNELS * HIDDEN + 2 * BATCH * POSITIONS * HIDDEN * OUT_COLS
 BYTES = (
@@ -67,6 +69,7 @@ def tile_classifiermodel_t_kernel(
         h_grouped = {}
         roi_tiles = {}
         planes = {}
+        logits = {}
 
         identity = const.tile([P, P], F32)
         conv_codes = const.tile([P, HIDDEN], U32, align_bytes=64)
@@ -240,8 +243,7 @@ def tile_classifiermodel_t_kernel(
             )
             planes[m] = result
 
-        def epilogue(m):
-            result = planes[m]
+        def collect_sums(m):
             z = finish.tile([P, OUT_COLS], F32)
             nc.vector.tensor_tensor(
                 out=z[:, :MAIN_COLS], in0=main_sums[m][:], in1=out_bias[:, :MAIN_COLS], op=ALU.add
@@ -249,6 +251,11 @@ def tile_classifiermodel_t_kernel(
             nc.vector.tensor_tensor(
                 out=z[:, MAIN_COLS:], in0=tail_sums[:, m, :], in1=out_bias[:, MAIN_COLS:], op=ALU.add
             )
+            logits[m] = z
+
+        def epilogue(m):
+            result = planes[m]
+            z = logits[m]
             c0 = z[:, 0:PROPOSALS]
             c1 = z[:, PROPOSALS : 2 * PROPOSALS]
             b1 = z[:, 2 * PROPOSALS : 3 * PROPOSALS]
@@ -265,70 +272,90 @@ def tile_classifiermodel_t_kernel(
                 out=growth[:].rearrange("p j q -> p (j q)"), in_=b23, func=ACT.Exp
             )
             shift = finish.tile([P, PROPOSALS], F32)
-            nc.vector.tensor_mul(out=shift[:], in0=b1, in1=result[:, 3, :])
-            nc.vector.tensor_sub(out=result[:, 0, :], in0=result[:, 0, :], in1=shift[:])
-            nc.vector.tensor_scalar(
+            nc.gpsimd.tensor_tensor(out=shift[:], in0=b1, in1=result[:, 3, :], op=ALU.mult)
+            nc.gpsimd.tensor_tensor(
+                out=result[:, 0, :], in0=result[:, 0, :], in1=shift[:], op=ALU.subtract
+            )
+            nc.gpsimd.tensor_scalar(
                 out=result[:, 4, :], in0=halfway[:], scalar1=0.5, scalar2=0.5, op0=ALU.mult, op1=ALU.add
             )
-            nc.vector.tensor_mul(out=result[:, 2:4, :], in0=result[:, 2:4, :], in1=growth[:])
+            nc.gpsimd.tensor_tensor(
+                out=result[:, 2:4, :], in0=result[:, 2:4, :], in1=growth[:], op=ALU.mult
+            )
+
+        def store_boxes(m):
             boxes = finish.tile([P, PROPOSALS, 5], F32)
-            nc.scalar.copy(out=boxes[:], in_=result[:].rearrange("p k q -> p q k"))
+            nc.scalar.copy(out=boxes[:], in_=planes[m][:].rearrange("p k q -> p q k"))
             nc.sync.dma_start(out=out[m * P : (m + 1) * P, :, :], in_=boxes[:])
 
-        masks.make_identity(nc, identity[:])
-        conv_raw = const.tile([P, PACK, HIDDEN], BF16)
-        nc.sync.dma_start(
-            out=conv_raw[:].rearrange("p (u e) d -> p u (e d)", e=2),
-            in_=conv_w.rearrange("(u p e) d -> p u (e d)", p=P, e=2),
-        )
-        conv_bias_raw = const.tile([P, HALVES], BF16)
-        nc.sync.dma_start(out=conv_bias_raw[:], in_=conv_b.rearrange("(p e) -> p e", e=HALVES))
-        load_slab(0)
-        for r in range(UNITS_AHEAD):
-            load_unit(r)
-        load_slab(1)
-        nc.sync.dma_start(out=out_bias[:, :CLS_COLS], in_=cls_b.partition_broadcast(P))
-        nc.sync.dma_start(out=out_bias[:, CLS_COLS:], in_=bbox_b[PROPOSALS:].partition_broadcast(P))
+        def load_out_bias():
+            nc.sync.dma_start(out=out_bias[:, :CLS_COLS], in_=cls_b.partition_broadcast(P))
+            nc.sync.dma_start(
+                out=out_bias[:, CLS_COLS:], in_=bbox_b[PROPOSALS:].partition_broadcast(P)
+            )
 
-        conv_grouped = const.tile([P, HALVES, P, PACK], BF16, align_bytes=64)
-        nc.vector.tensor_copy(
-            out=conv_grouped[:], in_=conv_raw[:].rearrange("p t (j h) -> p h j t", h=HALVES)
-        )
-        nc.vector.tensor_copy(out=conv_bias[:], in_=conv_bias_raw[:])
-        nc.vector.quantize_mx(
-            out=conv_codes[:].bitcast(FP8X4),
-            scales=conv_scales[:],
-            in_=conv_grouped[:].rearrange("p h j t -> p (h j t)"),
-        )
-        for piece in range(4):
-            regroup_weights(0, piece)
-            if piece % 2 == 1:
-                quantise_weights(0, piece // 2)
+        def prepare_conv():
+            conv_raw = const.tile([P, PACK, HIDDEN], BF16)
+            nc.sync.dma_start(
+                out=conv_raw[:].rearrange("p (u e) d -> p u (e d)", e=2),
+                in_=conv_w.rearrange("(u p e) d -> p u (e d)", p=P, e=2),
+            )
+            conv_bias_raw = const.tile([P, HALVES], BF16)
+            nc.sync.dma_start(out=conv_bias_raw[:], in_=conv_b.rearrange("(p e) -> p e", e=HALVES))
+            conv_grouped = const.tile([P, HALVES, P, PACK], BF16, align_bytes=64)
+            nc.vector.tensor_copy(
+                out=conv_grouped[:], in_=conv_raw[:].rearrange("p t (j h) -> p h j t", h=HALVES)
+            )
+            nc.vector.tensor_copy(out=conv_bias[:], in_=conv_bias_raw[:])
+            nc.vector.quantize_mx(
+                out=conv_codes[:].bitcast(FP8X4),
+                scales=conv_scales[:],
+                in_=conv_grouped[:].rearrange("p h j t -> p (h j t)"),
+            )
 
-        for r in range(ROUNDS + 2):
-            step, m = divmod(r, CHUNKS)
-            if r + UNITS_AHEAD < ROUNDS:
-                load_unit(r + UNITS_AHEAD)
-            if m == 0 and step + 2 < STEPS:
-                load_slab(step + 2)
-            if step == STEPS - 2:
-                load_roi(m)
-            if r >= 2:
-                quantise_hidden(r - 2)
-            if r < ROUNDS:
-                transpose_unit(r)
-            if step + 1 < STEPS:
-                regroup_weights(step + 1, m)
-            if step == STEPS - 1:
-                scale_roi(m)
-            if 1 <= r <= ROUNDS:
-                first_stage(r - 1)
-            if r < ROUNDS:
-                quantise_features(r)
-            if r >= 2:
-                second_stage(r - 2)
-            if step + 1 < STEPS and m % 2 == 1:
-                quantise_weights(step + 1, m // 2)
-            if r - 2 >= ROUNDS - CHUNKS:
-                tail_group(r - 2 - (ROUNDS - CHUNKS))
-                epilogue(r - 2 - (ROUNDS - CHUNKS))
+        with tc.manual_schedule():
+            masks.make_identity(nc, identity[:])
+            prepare_conv()
+            load_slab(0)
+            load_unit(0)
+            load_unit(1)
+            load_slab(1)
+            load_unit(2)
+            load_unit(3)
+
+            last_step = ROUNDS - CHUNKS
+            for r in range(-WEIGHTS_AHEAD, ROUNDS + 4):
+                step, m = divmod(r, CHUNKS)
+                if 0 <= r < ROUNDS - UNITS_AHEAD:
+                    load_unit(r + UNITS_AHEAD)
+                if 0 <= step < STEPS - 2 and m == 1:
+                    load_slab(step + 2)
+                if r == last_step - CHUNKS:
+                    load_out_bias()
+                if step == STEPS - 2:
+                    load_roi(m)
+                if 0 <= r - 1 < ROUNDS:
+                    quantise_features(r - 1)
+                if 0 <= r - 2 < ROUNDS:
+                    quantise_hidden(r - 2)
+                if last_step <= r - 3 < ROUNDS:
+                    collect_sums(r - 3 - last_step)
+                if 0 <= r < ROUNDS:
+                    transpose_unit(r)
+                if 0 <= r - 1 < ROUNDS:
+                    first_stage(r - 1)
+                if 0 <= r - 2 < ROUNDS:
+                    second_stage(r - 2)
+                if last_step <= r - 2 < ROUNDS:
+                    tail_group(r - 2 - last_step)
+                piece = r + WEIGHTS_AHEAD
+                if 0 <= piece - 1 < STEPS * PIECES and (piece - 1) % 2 == 1:
+                    quantise_weights((piece - 1) // PIECES, ((piece - 1) % PIECES) // 2)
+                if piece < STEPS * PIECES:
+                    regroup_weights(piece // PIECES, piece % PIECES)
+                if step == STEPS - 1:
+                    scale_roi(m)
+                if last_step <= r - 4 < ROUNDS:
+                    store_boxes(r - 4 - last_step)
+                if last_step <= r - 3 < ROUNDS:
+                    epilogue(r - 3 - last_step)

@@ -57,7 +57,7 @@ def tile_classifiermodel_t_kernel(
         weights = stack.enter_context(tc.tile_pool(name="weights", bufs=2))
         finish = stack.enter_context(tc.tile_pool(name="finish", bufs=2))
         planes_pool = stack.enter_context(tc.tile_pool(name="planes", bufs=CHUNKS))
-        work = stack.enter_context(tc.psum_pool(name="work", bufs=3))
+        work = stack.enter_context(tc.psum_pool(name="work", bufs=4))
         sums = stack.enter_context(tc.psum_pool(name="sums", bufs=1))
 
         x_tiles = {}
@@ -70,6 +70,7 @@ def tile_classifiermodel_t_kernel(
         roi_tiles = {}
         planes = {}
         logits = {}
+        tail_tiles = {}
 
         identity = const.tile([P, P], F32)
         conv_codes = const.tile([P, HIDDEN], U32, align_bytes=64)
@@ -81,7 +82,6 @@ def tile_classifiermodel_t_kernel(
         tail_codes = const.tile([P, STEPS, HALVES, TAIL_COLS], U32, align_bytes=64)
         tail_scales = const.tile([P, STEPS, HALVES, TAIL_COLS], U8, align_bytes=64)
         main_sums = [sums.tile([P, MAIN_COLS], F32, name="main_sum%d" % m) for m in range(CHUNKS)]
-        tail_sums = sums.tile([P, CHUNKS, TAIL_COLS], F32)
 
         def load_unit(r):
             step, m = divmod(r, CHUNKS)
@@ -214,6 +214,10 @@ def tile_classifiermodel_t_kernel(
                 )
 
         def tail_group(m):
+            if m == 0:
+                tail_bank = work.tile([P, CHUNKS, TAIL_COLS], F32, tag="work")
+                tail_tiles[0] = tail_bank
+            tail_sums = tail_tiles[0]
             images = slice(m * P, (m + 1) * P)
             for step in range(STEPS):
                 for e in range(HALVES):
@@ -249,7 +253,7 @@ def tile_classifiermodel_t_kernel(
                 out=z[:, :MAIN_COLS], in0=main_sums[m][:], in1=out_bias[:, :MAIN_COLS], op=ALU.add
             )
             nc.vector.tensor_tensor(
-                out=z[:, MAIN_COLS:], in0=tail_sums[:, m, :], in1=out_bias[:, MAIN_COLS:], op=ALU.add
+                out=z[:, MAIN_COLS:], in0=tail_tiles[0][:, m, :], in1=out_bias[:, MAIN_COLS:], op=ALU.add
             )
             logits[m] = z
 

@@ -31,7 +31,7 @@ TAIL_COLS = PROPOSALS
 OUT_COLS = MAIN_COLS + TAIL_COLS
 UNITS_AHEAD = 4
 PIECES = 4
-WEIGHTS_AHEAD = 3
+WEIGHTS_AHEAD = 1
 
 FLOPS = 2 * BATCH * POSITIONS * CHANNELS * HIDDEN + 2 * BATCH * POSITIONS * HIDDEN * OUT_COLS
 BYTES = (
@@ -53,7 +53,7 @@ def tile_classifiermodel_t_kernel(
         const = stack.enter_context(tc.tile_pool(name="const", bufs=1))
         x_pool = stack.enter_context(tc.tile_pool(name="x", bufs=UNITS_AHEAD + 2))
         raw_pool = stack.enter_context(tc.tile_pool(name="raw", bufs=2))
-        stage = stack.enter_context(tc.tile_pool(name="stage", bufs=3))
+        stage = stack.enter_context(tc.tile_pool(name="stage", bufs=4))
         weights = stack.enter_context(tc.tile_pool(name="weights", bufs=2))
         finish = stack.enter_context(tc.tile_pool(name="finish", bufs=2))
         planes_pool = stack.enter_context(tc.tile_pool(name="planes", bufs=CHUNKS))
@@ -69,16 +69,16 @@ def tile_classifiermodel_t_kernel(
         h_grouped = {}
         roi_tiles = {}
         planes = {}
-        logits = {}
-        tail_tiles = {}
+        tail_sums = {}
+        activated = {}
 
         identity = const.tile([P, P], F32)
         conv_codes = const.tile([P, HIDDEN], U32, align_bytes=64)
         conv_scales = const.tile([P, HIDDEN], U8, align_bytes=64)
         conv_bias = const.tile([P, HALVES], F32)
         out_bias = const.tile([P, OUT_COLS], BF16)
-        h_codes = const.tile([P, STEPS, HALVES, BATCH], U32, align_bytes=64)
-        h_scales = const.tile([P, STEPS, HALVES, BATCH], U8, align_bytes=64)
+        h_codes = const.tile([P, STEPS, CHUNKS, HALVES, P], U32, align_bytes=64)
+        h_scales = const.tile([P, STEPS, CHUNKS, HALVES, P], U8, align_bytes=64)
         tail_codes = const.tile([P, STEPS, HALVES, TAIL_COLS], U32, align_bytes=64)
         tail_scales = const.tile([P, STEPS, HALVES, TAIL_COLS], U8, align_bytes=64)
         main_sums = [sums.tile([P, MAIN_COLS], F32, name="main_sum%d" % m) for m in range(CHUNKS)]
@@ -190,46 +190,47 @@ def tile_classifiermodel_t_kernel(
 
         def quantise_hidden(r):
             step, m = divmod(r, CHUNKS)
-            images = slice(m * P, (m + 1) * P)
-            for e in range(HALVES):
-                nc.vector.quantize_mx(
-                    out=h_codes[:, step, e, images].bitcast(FP8X4),
-                    scales=h_scales[:, step, e, images],
-                    in_=h_grouped[r][:, e, :, :].rearrange("p b t -> p (b t)"),
-                )
+            nc.vector.quantize_mx(
+                out=h_codes[:, step, m, :, :].rearrange("p e b -> p (e b)").bitcast(FP8X4),
+                scales=h_scales[:, step, m, :, :].rearrange("p e b -> p (e b)"),
+                in_=h_grouped[r][:].rearrange("p e b t -> p (e b t)"),
+            )
 
         def second_stage(r):
             step, m = divmod(r, CHUNKS)
-            images = slice(m * P, (m + 1) * P)
             w_codes, w_scales = main_weights[step]
             for e in range(HALVES):
                 nc.tensor.matmul_mx(
                     out=main_sums[m][:],
-                    lhsT=h_codes[:, step, e, images].bitcast(FP8X4),
-                    lhsT_scale=h_scales[:, step, e, images],
+                    lhsT=h_codes[:, step, m, e, :].bitcast(FP8X4),
+                    lhsT_scale=h_scales[:, step, m, e, :],
                     rhs=w_codes[:, e, :].bitcast(FP8X4),
                     rhs_scale=w_scales[:, e, :],
                     start=(step == 0 and e == 0),
                     stop=(step == STEPS - 1 and e == HALVES - 1),
                 )
 
-        def tail_group(m):
-            if m == 0:
-                tail_bank = work.tile([P, CHUNKS, TAIL_COLS], F32, tag="work")
-                tail_tiles[0] = tail_bank
-            tail_sums = tail_tiles[0]
-            images = slice(m * P, (m + 1) * P)
-            for step in range(STEPS):
+        def tail_passes(m, steps):
+            if 0 in steps:
+                tail_sum = work.tile([P, TAIL_COLS], F32, tag="work")
+                tail_sums[m] = tail_sum
+            for step in steps:
                 for e in range(HALVES):
                     nc.tensor.matmul_mx(
-                        out=tail_sums[:, m, :],
-                        lhsT=h_codes[:, step, e, images].bitcast(FP8X4),
-                        lhsT_scale=h_scales[:, step, e, images],
+                        out=tail_sums[m][:],
+                        lhsT=h_codes[:, step, m, e, :].bitcast(FP8X4),
+                        lhsT_scale=h_scales[:, step, m, e, :],
                         rhs=tail_codes[:, step, e, :].bitcast(FP8X4),
                         rhs_scale=tail_scales[:, step, e, :],
                         start=(step == 0 and e == 0),
                         stop=(step == STEPS - 1 and e == HALVES - 1),
                     )
+
+        def load_out_bias():
+            nc.sync.dma_start(out=out_bias[:, :CLS_COLS], in_=cls_b.partition_broadcast(P))
+            nc.sync.dma_start(
+                out=out_bias[:, CLS_COLS:], in_=bbox_b[PROPOSALS:].partition_broadcast(P)
+            )
 
         def load_roi(m):
             roi_raw = planes_pool.tile([P, PROPOSALS * 4], BF16)
@@ -247,19 +248,15 @@ def tile_classifiermodel_t_kernel(
             )
             planes[m] = result
 
-        def collect_sums(m):
+        def activate_sums(m):
+            result = planes[m]
             z = finish.tile([P, OUT_COLS], F32)
             nc.vector.tensor_tensor(
                 out=z[:, :MAIN_COLS], in0=main_sums[m][:], in1=out_bias[:, :MAIN_COLS], op=ALU.add
             )
             nc.vector.tensor_tensor(
-                out=z[:, MAIN_COLS:], in0=tail_tiles[0][:, m, :], in1=out_bias[:, MAIN_COLS:], op=ALU.add
+                out=z[:, MAIN_COLS:], in0=tail_sums[m][:], in1=out_bias[:, MAIN_COLS:], op=ALU.add
             )
-            logits[m] = z
-
-        def epilogue(m):
-            result = planes[m]
-            z = logits[m]
             c0 = z[:, 0:PROPOSALS]
             c1 = z[:, PROPOSALS : 2 * PROPOSALS]
             b1 = z[:, 2 * PROPOSALS : 3 * PROPOSALS]
@@ -280,23 +277,18 @@ def tile_classifiermodel_t_kernel(
             nc.gpsimd.tensor_tensor(
                 out=result[:, 0, :], in0=result[:, 0, :], in1=shift[:], op=ALU.subtract
             )
-            nc.gpsimd.tensor_scalar(
-                out=result[:, 4, :], in0=halfway[:], scalar1=0.5, scalar2=0.5, op0=ALU.mult, op1=ALU.add
-            )
-            nc.gpsimd.tensor_tensor(
-                out=result[:, 2:4, :], in0=result[:, 2:4, :], in1=growth[:], op=ALU.mult
-            )
+            activated[m] = (halfway, growth)
 
         def store_boxes(m):
-            boxes = finish.tile([P, PROPOSALS, 5], F32)
-            nc.scalar.copy(out=boxes[:], in_=planes[m][:].rearrange("p k q -> p q k"))
-            nc.sync.dma_start(out=out[m * P : (m + 1) * P, :, :], in_=boxes[:])
-
-        def load_out_bias():
-            nc.sync.dma_start(out=out_bias[:, :CLS_COLS], in_=cls_b.partition_broadcast(P))
-            nc.sync.dma_start(
-                out=out_bias[:, CLS_COLS:], in_=bbox_b[PROPOSALS:].partition_broadcast(P)
+            result = planes[m]
+            halfway, growth = activated[m]
+            nc.vector.tensor_scalar(
+                out=result[:, 4, :], in0=halfway[:], scalar1=0.5, scalar2=0.5, op0=ALU.mult, op1=ALU.add
             )
+            nc.vector.tensor_mul(out=result[:, 2:4, :], in0=result[:, 2:4, :], in1=growth[:])
+            boxes = finish.tile([P, PROPOSALS, 5], F32)
+            nc.scalar.copy(out=boxes[:], in_=result[:].rearrange("p k q -> p q k"))
+            nc.sync.dma_start(out=out[m * P : (m + 1) * P, :, :], in_=boxes[:])
 
         def prepare_conv():
             conv_raw = const.tile([P, PACK, HIDDEN], BF16)
@@ -320,19 +312,19 @@ def tile_classifiermodel_t_kernel(
         with tc.manual_schedule():
             masks.make_identity(nc, identity[:])
             prepare_conv()
-            load_slab(0)
             load_unit(0)
             load_unit(1)
-            load_slab(1)
+            load_slab(0)
             load_unit(2)
             load_unit(3)
+            load_slab(1)
 
             last_step = ROUNDS - CHUNKS
-            for r in range(-WEIGHTS_AHEAD, ROUNDS + 4):
+            for r in range(-WEIGHTS_AHEAD, ROUNDS + 7):
                 step, m = divmod(r, CHUNKS)
                 if 0 <= r < ROUNDS - UNITS_AHEAD:
                     load_unit(r + UNITS_AHEAD)
-                if 0 <= step < STEPS - 2 and m == 1:
+                if 0 <= step < STEPS - 2 and m == CHUNKS - 1:
                     load_slab(step + 2)
                 if r == last_step - CHUNKS:
                     load_out_bias()
@@ -340,18 +332,18 @@ def tile_classifiermodel_t_kernel(
                     load_roi(m)
                 if 0 <= r - 1 < ROUNDS:
                     quantise_features(r - 1)
-                if 0 <= r - 2 < ROUNDS:
-                    quantise_hidden(r - 2)
-                if last_step <= r - 3 < ROUNDS:
-                    collect_sums(r - 3 - last_step)
+                if 0 <= r - 3 < ROUNDS:
+                    quantise_hidden(r - 3)
                 if 0 <= r < ROUNDS:
                     transpose_unit(r)
-                if 0 <= r - 1 < ROUNDS:
-                    first_stage(r - 1)
                 if 0 <= r - 2 < ROUNDS:
-                    second_stage(r - 2)
-                if last_step <= r - 2 < ROUNDS:
-                    tail_group(r - 2 - last_step)
+                    first_stage(r - 2)
+                if last_step <= r - 4 < ROUNDS:
+                    tail_passes(r - 4 - last_step, range(STEPS - 1))
+                if 0 <= r - 4 < ROUNDS:
+                    second_stage(r - 4)
+                if last_step <= r - 4 < ROUNDS:
+                    tail_passes(r - 4 - last_step, range(STEPS - 1, STEPS))
                 piece = r + WEIGHTS_AHEAD
                 if 0 <= piece - 1 < STEPS * PIECES and (piece - 1) % 2 == 1:
                     quantise_weights((piece - 1) // PIECES, ((piece - 1) % PIECES) // 2)
@@ -359,7 +351,7 @@ def tile_classifiermodel_t_kernel(
                     regroup_weights(piece // PIECES, piece % PIECES)
                 if step == STEPS - 1:
                     scale_roi(m)
-                if last_step <= r - 4 < ROUNDS:
-                    store_boxes(r - 4 - last_step)
-                if last_step <= r - 3 < ROUNDS:
-                    epilogue(r - 3 - last_step)
+                if last_step <= r - 6 < ROUNDS:
+                    store_boxes(r - 6 - last_step)
+                if last_step <= r - 5 < ROUNDS:
+                    activate_sums(r - 5 - last_step)

@@ -21,17 +21,27 @@ PROPOSALS = 128
 STRIDE = 16.0
 
 CHUNKS = BATCH // P
+LAST = CHUNKS - 1
 STEPS = POSITIONS // PACK
-ROUNDS = STEPS * CHUNKS
 HALVES = HIDDEN // P
 CLS_COLS = 2 * PROPOSALS
 BOX_COLS = 3 * PROPOSALS
 MAIN_COLS = 512
 TAIL_COLS = PROPOSALS
 OUT_COLS = MAIN_COLS + TAIL_COLS
-UNITS_AHEAD = 4
-PIECES = 4
-WEIGHTS_AHEAD = 1
+LAG = 0
+VECTOR_RELUS = 0
+SHARE = 48
+AHEAD = 6
+
+UNITS = [
+    (t - LAG * (m == LAST), m)
+    for t in range(STEPS + LAG)
+    for m in range(CHUNKS)
+    if 0 <= t - LAG * (m == LAST) < STEPS
+]
+ROUNDS = len(UNITS)
+FIRST_USE = [UNITS.index((step, 0)) for step in range(STEPS)]
 
 FLOPS = 2 * BATCH * POSITIONS * CHANNELS * HIDDEN + 2 * BATCH * POSITIONS * HIDDEN * OUT_COLS
 BYTES = (
@@ -51,9 +61,9 @@ def tile_classifiermodel_t_kernel(
 
     with ExitStack() as stack:
         const = stack.enter_context(tc.tile_pool(name="const", bufs=1))
-        x_pool = stack.enter_context(tc.tile_pool(name="x", bufs=UNITS_AHEAD + 2))
-        raw_pool = stack.enter_context(tc.tile_pool(name="raw", bufs=2))
-        stage = stack.enter_context(tc.tile_pool(name="stage", bufs=4))
+        x_pool = stack.enter_context(tc.tile_pool(name="x", bufs=AHEAD + 1))
+        raw_pool = stack.enter_context(tc.tile_pool(name="raw", bufs=3))
+        stage = stack.enter_context(tc.tile_pool(name="stage", bufs=3))
         weights = stack.enter_context(tc.tile_pool(name="weights", bufs=2))
         finish = stack.enter_context(tc.tile_pool(name="finish", bufs=2))
         planes_pool = stack.enter_context(tc.tile_pool(name="planes", bufs=CHUNKS))
@@ -61,9 +71,9 @@ def tile_classifiermodel_t_kernel(
         sums = stack.enter_context(tc.psum_pool(name="sums", bufs=1))
 
         x_tiles = {}
-        raw_tiles = {}
+        cls_tiles = {}
+        box_tiles = {}
         grouped_weights = {}
-        main_weights = {}
         x_grouped = {}
         x_quantised = {}
         h_grouped = {}
@@ -73,46 +83,63 @@ def tile_classifiermodel_t_kernel(
         activated = {}
 
         identity = const.tile([P, P], F32)
+        ones = const.tile([P, P], BF16)
+        bias_row = const.tile([P, OUT_COLS], BF16)
         conv_codes = const.tile([P, HIDDEN], U32, align_bytes=64)
         conv_scales = const.tile([P, HIDDEN], U8, align_bytes=64)
         conv_bias = const.tile([P, HALVES], F32)
-        out_bias = const.tile([P, OUT_COLS], BF16)
+        out_bias = const.tile([P, OUT_COLS], F32)
         h_codes = const.tile([P, STEPS, CHUNKS, HALVES, P], U32, align_bytes=64)
         h_scales = const.tile([P, STEPS, CHUNKS, HALVES, P], U8, align_bytes=64)
+        main_codes = const.tile([P, STEPS, HALVES, MAIN_COLS], U32, align_bytes=64)
+        main_scales = const.tile([P, STEPS, HALVES, MAIN_COLS], U8, align_bytes=64)
         tail_codes = const.tile([P, STEPS, HALVES, TAIL_COLS], U32, align_bytes=64)
         tail_scales = const.tile([P, STEPS, HALVES, TAIL_COLS], U8, align_bytes=64)
         main_sums = [sums.tile([P, MAIN_COLS], F32, name="main_sum%d" % m) for m in range(CHUNKS)]
 
         def load_unit(r):
-            step, m = divmod(r, CHUNKS)
+            step, m = UNITS[r]
             x = x_pool.tile([P, PACK, CHANNELS], BF16)
-            nc.sync.dma_start(
-                out=x[:],
-                in_=feature_rows[m * P : (m + 1) * P, step * PACK : (step + 1) * PACK, :],
-            )
+            pieces = 2 if r == 0 else 1
+            width = PACK // pieces
+            for piece in range(pieces):
+                first = step * PACK + piece * width
+                nc.sync.dma_start(
+                    out=x[:, piece * width : (piece + 1) * width, :],
+                    in_=feature_rows[m * P : (m + 1) * P, first : first + width, :],
+                )
             x_tiles[r] = x
 
-        def load_slab(step):
-            positions = slice(step * PACK, (step + 1) * PACK)
+        def load_cls(step):
             cls_raw = raw_pool.tile([P, PACK, HALVES, CLS_COLS], BF16)
             nc.sync.dma_start(
-                out=cls_raw[:].rearrange("p t e n -> p t (e n)"), in_=cls_rows[:, positions, :]
+                out=cls_raw[:].rearrange("p t e n -> p t (e n)"),
+                in_=cls_rows[:, step * PACK : (step + 1) * PACK, :],
             )
-            box_raw = raw_pool.tile([P, PACK, HALVES, BOX_COLS], BF16)
-            for e in range(HALVES):
-                nc.sync.dma_start(
-                    out=box_raw[:, :, e, :], in_=box_rows[:, positions, e, PROPOSALS:]
-                )
-            raw_tiles[step] = (cls_raw, box_raw)
+            cls_tiles[step] = cls_raw
 
-        def regroup_weights(step, piece):
-            e, source = divmod(piece, 2)
-            if piece == 0:
+        def load_box(step, e):
+            if e == 0:
+                box_raw = raw_pool.tile([P, PACK, HALVES, BOX_COLS], BF16)
+                box_tiles[step] = box_raw
+            nc.sync.dma_start(
+                out=box_tiles[step][:, :, e, :],
+                in_=box_rows[:, step * PACK : (step + 1) * PACK, e, PROPOSALS:],
+            )
+
+        def load_roi(m):
+            roi_raw = planes_pool.tile([P, PROPOSALS * 4], BF16)
+            nc.sync.dma_start(
+                out=roi_raw[:], in_=roi[m * P : (m + 1) * P, :, :].rearrange("b q k -> b (q k)")
+            )
+            roi_tiles[m] = roi_raw
+
+        def regroup_weights(step, e, source):
+            if e == 0 and source == 0:
                 w_grouped = weights.tile([P, HALVES, OUT_COLS, PACK], BF16, align_bytes=64)
                 grouped_weights[step] = w_grouped
-            raw = raw_tiles[step][source]
-            first = source * CLS_COLS
-            width = (CLS_COLS, BOX_COLS)[source]
+            raw = (cls_tiles, box_tiles)[source][step]
+            first, width = ((BOX_COLS, CLS_COLS), (0, BOX_COLS))[source]
             nc.vector.tensor_copy(
                 out=grouped_weights[step][:, e, first : first + width, :].rearrange(
                     "p (c i) t -> p c t i", i=4
@@ -121,15 +148,10 @@ def tile_classifiermodel_t_kernel(
             )
 
         def quantise_weights(step, e):
-            if e == 0:
-                w_codes = weights.tile([P, HALVES, MAIN_COLS], U32, align_bytes=64)
-                w_scales = weights.tile([P, HALVES, MAIN_COLS], U8, align_bytes=64)
-                main_weights[step] = (w_codes, w_scales)
-            w_codes, w_scales = main_weights[step]
             w_grouped = grouped_weights[step]
             nc.vector.quantize_mx(
-                out=w_codes[:, e, :].bitcast(FP8X4),
-                scales=w_scales[:, e, :],
+                out=main_codes[:, step, e, :].bitcast(FP8X4),
+                scales=main_scales[:, step, e, :],
                 in_=w_grouped[:, e, :MAIN_COLS, :].rearrange("p n t -> p (n t)"),
             )
             nc.vector.quantize_mx(
@@ -165,7 +187,7 @@ def tile_classifiermodel_t_kernel(
             )
             x_quantised[r] = (x_codes, x_scales)
 
-        def first_stage(r):
+        def first_stage(r, vector_halves):
             x_codes, x_scales = x_quantised[r]
             hidden = stage.tile([P, HALVES, P, PACK], BF16, align_bytes=64)
             for e in range(HALVES):
@@ -179,17 +201,28 @@ def tile_classifiermodel_t_kernel(
                     start=True,
                     stop=True,
                 )
-                nc.scalar.activation(
-                    out=hidden[:, e, :, :],
-                    in_=h_sum[:].rearrange("p (t b) -> p b t", t=PACK),
-                    func=ACT.Relu,
-                    bias=conv_bias[:, e : e + 1],
-                    scale=1.0,
-                )
+                h_view = h_sum[:].rearrange("p (t b) -> p b t", t=PACK)
+                if e in vector_halves:
+                    nc.vector.tensor_scalar(
+                        out=hidden[:, e, :, :],
+                        in0=h_view,
+                        scalar1=conv_bias[:, e : e + 1],
+                        scalar2=0.0,
+                        op0=ALU.add,
+                        op1=ALU.max,
+                    )
+                else:
+                    nc.scalar.activation(
+                        out=hidden[:, e, :, :],
+                        in_=h_view,
+                        func=ACT.Relu,
+                        bias=conv_bias[:, e : e + 1],
+                        scale=1.0,
+                    )
             h_grouped[r] = hidden
 
         def quantise_hidden(r):
-            step, m = divmod(r, CHUNKS)
+            step, m = UNITS[r]
             nc.vector.quantize_mx(
                 out=h_codes[:, step, m, :, :].rearrange("p e b -> p (e b)").bitcast(FP8X4),
                 scales=h_scales[:, step, m, :, :].rearrange("p e b -> p (e b)"),
@@ -197,15 +230,14 @@ def tile_classifiermodel_t_kernel(
             )
 
         def second_stage(r):
-            step, m = divmod(r, CHUNKS)
-            w_codes, w_scales = main_weights[step]
+            step, m = UNITS[r]
             for e in range(HALVES):
                 nc.tensor.matmul_mx(
                     out=main_sums[m][:],
                     lhsT=h_codes[:, step, m, e, :].bitcast(FP8X4),
                     lhsT_scale=h_scales[:, step, m, e, :],
-                    rhs=w_codes[:, e, :].bitcast(FP8X4),
-                    rhs_scale=w_scales[:, e, :],
+                    rhs=main_codes[:, step, e, :].bitcast(FP8X4),
+                    rhs_scale=main_scales[:, step, e, :],
                     start=(step == 0 and e == 0),
                     stop=(step == STEPS - 1 and e == HALVES - 1),
                 )
@@ -226,78 +258,92 @@ def tile_classifiermodel_t_kernel(
                         stop=(step == STEPS - 1 and e == HALVES - 1),
                     )
 
-        def load_out_bias():
-            nc.sync.dma_start(out=out_bias[:, :CLS_COLS], in_=cls_b.partition_broadcast(P))
-            nc.sync.dma_start(
-                out=out_bias[:, CLS_COLS:], in_=bbox_b[PROPOSALS:].partition_broadcast(P)
-            )
-
-        def load_roi(m):
-            roi_raw = planes_pool.tile([P, PROPOSALS * 4], BF16)
-            nc.sync.dma_start(
-                out=roi_raw[:], in_=roi[m * P : (m + 1) * P, :, :].rearrange("b q k -> b (q k)")
-            )
-            roi_tiles[m] = roi_raw
-
-        def scale_roi(m):
+        def copy_y(m):
             result = planes_pool.tile([P, 5, PROPOSALS], F32)
-            nc.vector.tensor_scalar_mul(
-                out=result[:, 0:4, :],
-                in0=roi_tiles[m][:].rearrange("p (q k) -> p k q", k=4),
-                scalar1=STRIDE,
-            )
             planes[m] = result
+            nc.gpsimd.tensor_scalar(
+                out=result[:, 1, :],
+                in0=roi_tiles[m][:].rearrange("p (q k) -> p k q", k=4)[:, 1, :],
+                scalar1=STRIDE,
+                scalar2=0.0,
+                op0=ALU.mult,
+                op1=ALU.add,
+            )
 
         def activate_sums(m):
-            result = planes[m]
-            z = finish.tile([P, OUT_COLS], F32)
+            z = finish.tile([P, MAIN_COLS], F32)
             nc.vector.tensor_tensor(
-                out=z[:, :MAIN_COLS], in0=main_sums[m][:], in1=out_bias[:, :MAIN_COLS], op=ALU.add
+                out=z[:], in0=main_sums[m][:], in1=out_bias[:, :MAIN_COLS], op=ALU.add
             )
-            nc.vector.tensor_tensor(
-                out=z[:, MAIN_COLS:], in0=tail_sums[m][:], in1=out_bias[:, MAIN_COLS:], op=ALU.add
-            )
-            c0 = z[:, 0:PROPOSALS]
-            c1 = z[:, PROPOSALS : 2 * PROPOSALS]
-            b1 = z[:, 2 * PROPOSALS : 3 * PROPOSALS]
-            b23 = z[:, 3 * PROPOSALS :]
-            logit = finish.tile([P, PROPOSALS], F32)
-            nc.vector.tensor_sub(out=logit[:], in0=c1, in1=c0)
+            b23 = z[:, PROPOSALS:BOX_COLS]
             nc.vector.tensor_scalar(
                 out=b23, in0=b23, scalar1=-10.0, scalar2=10.0, op0=ALU.max, op1=ALU.min
             )
-            halfway = finish.tile([P, PROPOSALS], F32)
-            nc.scalar.activation(out=halfway[:], in_=logit[:], func=ACT.Tanh, scale=0.5)
+            logit = finish.tile([P, PROPOSALS], F32)
+            nc.vector.tensor_tensor(
+                out=logit[:], in0=tail_sums[m][:], in1=z[:, BOX_COLS:], op=ALU.subtract
+            )
+            activated[m] = (z, logit)
+
+        def exponentials(m):
+            result = planes[m]
+            roi_planes = roi_tiles[m][:].rearrange("p (q k) -> p k q", k=4)
+            z, logit = activated[m]
+            b1 = z[:, :PROPOSALS]
+            b23 = z[:, PROPOSALS:BOX_COLS]
             growth = finish.tile([P, 2, PROPOSALS], F32)
             nc.scalar.activation(
                 out=growth[:].rearrange("p j q -> p (j q)"), in_=b23, func=ACT.Exp
             )
+            halfway = finish.tile([P, PROPOSALS], F32)
+            nc.scalar.activation(out=halfway[:], in_=logit[:], func=ACT.Tanh, scale=0.5)
             shift = finish.tile([P, PROPOSALS], F32)
-            nc.gpsimd.tensor_tensor(out=shift[:], in0=b1, in1=result[:, 3, :], op=ALU.mult)
+            nc.gpsimd.tensor_tensor(out=shift[:], in0=b1, in1=roi_planes[:, 3, :], op=ALU.mult)
             nc.gpsimd.tensor_tensor(
-                out=result[:, 0, :], in0=result[:, 0, :], in1=shift[:], op=ALU.subtract
+                out=shift[:], in0=roi_planes[:, 0, :], in1=shift[:], op=ALU.subtract
+            )
+            nc.gpsimd.tensor_scalar(
+                out=result[:, 0, :], in0=shift[:], scalar1=STRIDE, scalar2=0.0,
+                op0=ALU.mult, op1=ALU.add,
             )
             activated[m] = (halfway, growth)
 
         def store_boxes(m):
             result = planes[m]
+            roi_planes = roi_tiles[m][:].rearrange("p (q k) -> p k q", k=4)
             halfway, growth = activated[m]
+            nc.vector.scalar_tensor_tensor(
+                out=result[:, 2:4, :],
+                in0=roi_planes[:, 2:4, :],
+                scalar=STRIDE,
+                in1=growth[:],
+                op0=ALU.mult,
+                op1=ALU.mult,
+            )
             nc.vector.tensor_scalar(
                 out=result[:, 4, :], in0=halfway[:], scalar1=0.5, scalar2=0.5, op0=ALU.mult, op1=ALU.add
             )
-            nc.vector.tensor_mul(out=result[:, 2:4, :], in0=result[:, 2:4, :], in1=growth[:])
             boxes = finish.tile([P, PROPOSALS, 5], F32)
-            nc.scalar.copy(out=boxes[:], in_=result[:].rearrange("p k q -> p q k"))
+            scalar_share = SHARE
+            if scalar_share:
+                nc.scalar.copy(
+                    out=boxes[:, :scalar_share, :],
+                    in_=result[:, :, :scalar_share].rearrange("p k q -> p q k"),
+                )
+            nc.vector.tensor_copy(
+                out=boxes[:, scalar_share:, :],
+                in_=result[:, :, scalar_share:].rearrange("p k q -> p q k"),
+            )
             nc.sync.dma_start(out=out[m * P : (m + 1) * P, :, :], in_=boxes[:])
 
         def prepare_conv():
             conv_raw = const.tile([P, PACK, HIDDEN], BF16)
-            nc.sync.dma_start(
+            nc.scalar.dma_start(
                 out=conv_raw[:].rearrange("p (u e) d -> p u (e d)", e=2),
                 in_=conv_w.rearrange("(u p e) d -> p u (e d)", p=P, e=2),
             )
             conv_bias_raw = const.tile([P, HALVES], BF16)
-            nc.sync.dma_start(out=conv_bias_raw[:], in_=conv_b.rearrange("(p e) -> p e", e=HALVES))
+            nc.scalar.dma_start(out=conv_bias_raw[:], in_=conv_b.rearrange("(p e) -> p e", e=HALVES))
             conv_grouped = const.tile([P, HALVES, P, PACK], BF16, align_bytes=64)
             nc.vector.tensor_copy(
                 out=conv_grouped[:], in_=conv_raw[:].rearrange("p t (j h) -> p h j t", h=HALVES)
@@ -309,49 +355,90 @@ def tile_classifiermodel_t_kernel(
                 in_=conv_grouped[:].rearrange("p h j t -> p (h j t)"),
             )
 
-        with tc.manual_schedule():
-            masks.make_identity(nc, identity[:])
-            prepare_conv()
-            load_unit(0)
-            load_unit(1)
-            load_slab(0)
-            load_unit(2)
-            load_unit(3)
-            load_slab(1)
+        def load_out_bias():
+            nc.scalar.dma_start(
+                out=bias_row[0:1, :BOX_COLS], in_=bbox_b[PROPOSALS:].rearrange("(a n) -> a n", a=1)
+            )
+            nc.scalar.dma_start(
+                out=bias_row[0:1, BOX_COLS:], in_=cls_b.rearrange("(a n) -> a n", a=1)
+            )
 
-            last_step = ROUNDS - CHUNKS
-            for r in range(-WEIGHTS_AHEAD, ROUNDS + 7):
-                step, m = divmod(r, CHUNKS)
-                if 0 <= r < ROUNDS - UNITS_AHEAD:
-                    load_unit(r + UNITS_AHEAD)
-                if 0 <= step < STEPS - 2 and m == CHUNKS - 1:
-                    load_slab(step + 2)
-                if r == last_step - CHUNKS:
-                    load_out_bias()
-                if step == STEPS - 2:
-                    load_roi(m)
+        def spread_out_bias():
+            for columns in (slice(0, MAIN_COLS), slice(MAIN_COLS, OUT_COLS)):
+                spread = work.tile([P, columns.stop - columns.start], F32, tag="work")
+                nc.tensor.matmul(
+                    out=spread[:], lhsT=ones[:], rhs=bias_row[:, columns], start=True, stop=True
+                )
+                nc.scalar.copy(out=out_bias[:, columns], in_=spread[:])
+            nc.vector.tensor_sub(
+                out=out_bias[:, BOX_COLS:MAIN_COLS],
+                in0=out_bias[:, BOX_COLS:MAIN_COLS],
+                in1=out_bias[:, MAIN_COLS:],
+            )
+
+        weight_tasks = {}
+        loads = [(r, 0, load_unit, (r,)) for r in range(ROUNDS)]
+        for step in range(STEPS):
+            first = FIRST_USE[step - 1] + 4 if step else 1
+            rounds = FIRST_USE[step] + 4 - first
+            tasks = [
+                (regroup_weights, (step, 0, 0)),
+                (regroup_weights, (step, 1, 0)),
+                (regroup_weights, (step, 0, 1)),
+                (quantise_weights, (step, 0)),
+                (regroup_weights, (step, 1, 1)),
+                (quantise_weights, (step, 1)),
+            ]
+            for i, task in enumerate(tasks):
+                weight_tasks.setdefault(first + i * rounds // len(tasks), []).append(task)
+            loads.append((first, 1, load_cls, (step,)))
+            loads.append((first + 1, 1, load_box, (step, 0)))
+            loads.append((first + 2, 1, load_box, (step, 1)))
+        loads.sort(key=lambda load: (load[0], load[1]))
+        last_unit = [UNITS.index((STEPS - 1, m)) for m in range(CHUNKS)]
+        roi_round = 12
+
+        with tc.manual_schedule():
+            nc.vector.memset(bias_row[:], 0.0)
+            nc.vector.memset(ones[:], 1.0)
+            masks.make_identity(nc, identity[:])
+            load_unit(0)
+            load_out_bias()
+            prepare_conv()
+            issued = 1
+            for r in range(ROUNDS + 8):
+                while issued < len(loads) and loads[issued][0] <= r + AHEAD:
+                    need, rank, load, arguments = loads[issued]
+                    load(*arguments)
+                    issued += 1
+                if 0 <= r - roi_round < CHUNKS:
+                    load_roi(r - roi_round)
+                for m in range(CHUNKS):
+                    if r == last_unit[m] + 5:
+                        activate_sums(m)
+                    if r == last_unit[m] + 6:
+                        exponentials(m)
+                    if r == last_unit[m] + 7:
+                        store_boxes(m)
+                tasks = weight_tasks.get(r, [])
                 if 0 <= r - 1 < ROUNDS:
                     quantise_features(r - 1)
+                for task, arguments in tasks:
+                    task(*arguments)
                 if 0 <= r - 3 < ROUNDS:
                     quantise_hidden(r - 3)
-                if 0 <= r < ROUNDS:
+                if r < ROUNDS:
                     transpose_unit(r)
                 if 0 <= r - 2 < ROUNDS:
-                    first_stage(r - 2)
-                if last_step <= r - 4 < ROUNDS:
-                    tail_passes(r - 4 - last_step, range(STEPS - 1))
+                    first_stage(r - 2, (1,) if r - 2 >= ROUNDS - VECTOR_RELUS else ())
                 if 0 <= r - 4 < ROUNDS:
                     second_stage(r - 4)
-                if last_step <= r - 4 < ROUNDS:
-                    tail_passes(r - 4 - last_step, range(STEPS - 1, STEPS))
-                piece = r + WEIGHTS_AHEAD
-                if 0 <= piece - 1 < STEPS * PIECES and (piece - 1) % 2 == 1:
-                    quantise_weights((piece - 1) // PIECES, ((piece - 1) % PIECES) // 2)
-                if piece < STEPS * PIECES:
-                    regroup_weights(piece // PIECES, piece % PIECES)
-                if step == STEPS - 1:
-                    scale_roi(m)
-                if last_step <= r - 6 < ROUNDS:
-                    store_boxes(r - 6 - last_step)
-                if last_step <= r - 5 < ROUNDS:
-                    activate_sums(r - 5 - last_step)
+                for m in range(CHUNKS):
+                    if r == last_unit[m] + 3:
+                        tail_passes(m, range(STEPS - 2))
+                    if r == last_unit[m] + 4:
+                        tail_passes(m, range(STEPS - 2, STEPS))
+                if r == 0:
+                    spread_out_bias()
+                if 0 <= r - roi_round - 3 < CHUNKS:
+                    copy_y(r - roi_round - 3)

@@ -27,8 +27,7 @@ HALVES = HIDDEN // P
 CLS_COLS = 2 * PROPOSALS
 BOX_COLS = 3 * PROPOSALS
 MAIN_COLS = 512
-TAIL_COLS = PROPOSALS
-OUT_COLS = MAIN_COLS + TAIL_COLS
+OUT_COLS = BOX_COLS + CLS_COLS
 LAG = 0
 VECTOR_RELUS = 0
 SHARE = 48
@@ -79,7 +78,6 @@ def tile_classifiermodel_t_kernel(
         h_grouped = {}
         roi_tiles = {}
         planes = {}
-        tail_sums = {}
         activated = {}
 
         identity = const.tile([P, P], F32)
@@ -88,13 +86,13 @@ def tile_classifiermodel_t_kernel(
         conv_codes = const.tile([P, HIDDEN], U32, align_bytes=64)
         conv_scales = const.tile([P, HIDDEN], U8, align_bytes=64)
         conv_bias = const.tile([P, HALVES], F32)
-        out_bias = const.tile([P, OUT_COLS], F32)
+        out_bias = const.tile([P, MAIN_COLS], F32)
         h_codes = const.tile([P, STEPS, CHUNKS, HALVES, P], U32, align_bytes=64)
         h_scales = const.tile([P, STEPS, CHUNKS, HALVES, P], U8, align_bytes=64)
         main_codes = const.tile([P, STEPS, HALVES, MAIN_COLS], U32, align_bytes=64)
         main_scales = const.tile([P, STEPS, HALVES, MAIN_COLS], U8, align_bytes=64)
-        tail_codes = const.tile([P, STEPS, HALVES, TAIL_COLS], U32, align_bytes=64)
-        tail_scales = const.tile([P, STEPS, HALVES, TAIL_COLS], U8, align_bytes=64)
+        minus_codes = const.tile([P, STEPS, HALVES, PROPOSALS], U32, align_bytes=64)
+        minus_scales = const.tile([P, STEPS, HALVES, PROPOSALS], U8, align_bytes=64)
         main_sums = [sums.tile([P, MAIN_COLS], F32, name="main_sum%d" % m) for m in range(CHUNKS)]
 
         def load_unit(r):
@@ -134,30 +132,46 @@ def tile_classifiermodel_t_kernel(
             )
             roi_tiles[m] = roi_raw
 
-        def regroup_weights(step, e, source):
-            if e == 0 and source == 0:
-                w_grouped = weights.tile([P, HALVES, OUT_COLS, PACK], BF16, align_bytes=64)
-                grouped_weights[step] = w_grouped
-            raw = (cls_tiles, box_tiles)[source][step]
-            first, width = ((BOX_COLS, CLS_COLS), (0, BOX_COLS))[source]
-            nc.vector.tensor_copy(
-                out=grouped_weights[step][:, e, first : first + width, :].rearrange(
-                    "p (c i) t -> p c t i", i=4
-                ),
-                in_=raw[:, :, e, :].rearrange("p t (c i) -> p c t i", i=4),
+        def open_weights(step):
+            w_grouped = weights.tile([P, HALVES, MAIN_COLS, PACK], BF16, align_bytes=64)
+            w_minus = weights.tile([P, HALVES, PROPOSALS, PACK], BF16, align_bytes=64)
+            grouped_weights[step] = (w_grouped, w_minus)
+
+        def regroup_minus(step, e):
+            nc.vector.tensor_scalar_mul(
+                out=grouped_weights[step][1][:, e, :, :].rearrange("p (c i) t -> p c t i", i=4),
+                in0=cls_tiles[step][:, :, e, :PROPOSALS].rearrange("p t (c i) -> p c t i", i=4),
+                scalar1=-1.0,
             )
 
-        def quantise_weights(step, e):
-            w_grouped = grouped_weights[step]
+        def regroup_plus(step, e):
+            nc.vector.tensor_copy(
+                out=grouped_weights[step][0][:, e, BOX_COLS:, :].rearrange(
+                    "p (c i) t -> p c t i", i=4
+                ),
+                in_=cls_tiles[step][:, :, e, PROPOSALS:].rearrange("p t (c i) -> p c t i", i=4),
+            )
+
+        def regroup_box(step, e):
+            nc.vector.tensor_copy(
+                out=grouped_weights[step][0][:, e, :BOX_COLS, :].rearrange(
+                    "p (c i) t -> p c t i", i=4
+                ),
+                in_=box_tiles[step][:, :, e, :].rearrange("p t (c i) -> p c t i", i=4),
+            )
+
+        def quantise_main(step, e):
             nc.vector.quantize_mx(
                 out=main_codes[:, step, e, :].bitcast(FP8X4),
                 scales=main_scales[:, step, e, :],
-                in_=w_grouped[:, e, :MAIN_COLS, :].rearrange("p n t -> p (n t)"),
+                in_=grouped_weights[step][0][:, e, :, :].rearrange("p n t -> p (n t)"),
             )
+
+        def quantise_minus(step):
             nc.vector.quantize_mx(
-                out=tail_codes[:, step, e, :].bitcast(FP8X4),
-                scales=tail_scales[:, step, e, :],
-                in_=w_grouped[:, e, MAIN_COLS:, :].rearrange("p n t -> p (n t)"),
+                out=minus_codes[:, step, :, :].rearrange("p e n -> p (e n)").bitcast(FP8X4),
+                scales=minus_scales[:, step, :, :].rearrange("p e n -> p (e n)"),
+                in_=grouped_weights[step][1][:].rearrange("p e n t -> p (e n t)"),
             )
 
         def transpose_unit(r):
@@ -232,31 +246,30 @@ def tile_classifiermodel_t_kernel(
         def second_stage(r):
             step, m = UNITS[r]
             for e in range(HALVES):
-                nc.tensor.matmul_mx(
-                    out=main_sums[m][:],
-                    lhsT=h_codes[:, step, m, e, :].bitcast(FP8X4),
-                    lhsT_scale=h_scales[:, step, m, e, :],
-                    rhs=main_codes[:, step, e, :].bitcast(FP8X4),
-                    rhs_scale=main_scales[:, step, e, :],
-                    start=(step == 0 and e == 0),
-                    stop=(step == STEPS - 1 and e == HALVES - 1),
-                )
-
-        def tail_passes(m, steps):
-            if 0 in steps:
-                tail_sum = work.tile([P, TAIL_COLS], F32, tag="work")
-                tail_sums[m] = tail_sum
-            for step in steps:
-                for e in range(HALVES):
+                def main_pass():
                     nc.tensor.matmul_mx(
-                        out=tail_sums[m][:],
+                        out=main_sums[m][:],
                         lhsT=h_codes[:, step, m, e, :].bitcast(FP8X4),
                         lhsT_scale=h_scales[:, step, m, e, :],
-                        rhs=tail_codes[:, step, e, :].bitcast(FP8X4),
-                        rhs_scale=tail_scales[:, step, e, :],
+                        rhs=main_codes[:, step, e, :].bitcast(FP8X4),
+                        rhs_scale=main_scales[:, step, e, :],
                         start=(step == 0 and e == 0),
                         stop=(step == STEPS - 1 and e == HALVES - 1),
                     )
+
+                def minus_pass():
+                    nc.tensor.matmul_mx(
+                        out=main_sums[m][:, BOX_COLS:],
+                        lhsT=h_codes[:, step, m, e, :].bitcast(FP8X4),
+                        lhsT_scale=h_scales[:, step, m, e, :],
+                        rhs=minus_codes[:, step, e, :].bitcast(FP8X4),
+                        rhs_scale=minus_scales[:, step, e, :],
+                        start=False,
+                        stop=False,
+                    )
+
+                for one_pass in (main_pass, minus_pass) if e == 0 else (minus_pass, main_pass):
+                    one_pass()
 
         def copy_y(m):
             result = planes_pool.tile([P, 5, PROPOSALS], F32)
@@ -272,23 +285,18 @@ def tile_classifiermodel_t_kernel(
 
         def activate_sums(m):
             z = finish.tile([P, MAIN_COLS], F32)
-            nc.vector.tensor_tensor(
-                out=z[:], in0=main_sums[m][:], in1=out_bias[:, :MAIN_COLS], op=ALU.add
-            )
+            nc.vector.tensor_tensor(out=z[:], in0=main_sums[m][:], in1=out_bias[:], op=ALU.add)
             b23 = z[:, PROPOSALS:BOX_COLS]
             nc.vector.tensor_scalar(
                 out=b23, in0=b23, scalar1=-10.0, scalar2=10.0, op0=ALU.max, op1=ALU.min
             )
-            logit = finish.tile([P, PROPOSALS], F32)
-            nc.vector.tensor_tensor(
-                out=logit[:], in0=tail_sums[m][:], in1=z[:, BOX_COLS:], op=ALU.subtract
-            )
-            activated[m] = (z, logit)
+            activated[m] = z
 
         def exponentials(m):
             result = planes[m]
             roi_planes = roi_tiles[m][:].rearrange("p (q k) -> p k q", k=4)
-            z, logit = activated[m]
+            z = activated[m]
+            logit = z[:, BOX_COLS:]
             b1 = z[:, :PROPOSALS]
             b23 = z[:, PROPOSALS:BOX_COLS]
             growth = finish.tile([P, 2, PROPOSALS], F32)
@@ -296,7 +304,7 @@ def tile_classifiermodel_t_kernel(
                 out=growth[:].rearrange("p j q -> p (j q)"), in_=b23, func=ACT.Exp
             )
             halfway = finish.tile([P, PROPOSALS], F32)
-            nc.scalar.activation(out=halfway[:], in_=logit[:], func=ACT.Tanh, scale=0.5)
+            nc.scalar.activation(out=halfway[:], in_=logit, func=ACT.Tanh, scale=0.5)
             shift = finish.tile([P, PROPOSALS], F32)
             nc.gpsimd.tensor_tensor(out=shift[:], in0=b1, in1=roi_planes[:, 3, :], op=ALU.mult)
             nc.gpsimd.tensor_tensor(
@@ -364,17 +372,21 @@ def tile_classifiermodel_t_kernel(
             )
 
         def spread_out_bias():
-            for columns in (slice(0, MAIN_COLS), slice(MAIN_COLS, OUT_COLS)):
+            for i, columns in enumerate((slice(BOX_COLS, OUT_COLS), slice(0, BOX_COLS))):
                 spread = work.tile([P, columns.stop - columns.start], F32, tag="work")
                 nc.tensor.matmul(
                     out=spread[:], lhsT=ones[:], rhs=bias_row[:, columns], start=True, stop=True
                 )
-                nc.scalar.copy(out=out_bias[:, columns], in_=spread[:])
-            nc.vector.tensor_sub(
-                out=out_bias[:, BOX_COLS:MAIN_COLS],
-                in0=out_bias[:, BOX_COLS:MAIN_COLS],
-                in1=out_bias[:, MAIN_COLS:],
-            )
+                if i:
+                    nc.scalar.copy(out=out_bias[:, :BOX_COLS], in_=spread[:])
+                else:
+                    cls_bias = const.tile([P, CLS_COLS], F32)
+                    nc.scalar.copy(out=cls_bias[:], in_=spread[:])
+                    nc.vector.tensor_sub(
+                        out=out_bias[:, BOX_COLS:],
+                        in0=cls_bias[:, PROPOSALS:],
+                        in1=cls_bias[:, :PROPOSALS],
+                    )
 
         weight_tasks = {}
         loads = [(r, 0, load_unit, (r,)) for r in range(ROUNDS)]
@@ -382,12 +394,16 @@ def tile_classifiermodel_t_kernel(
             first = FIRST_USE[step - 1] + 4 if step else 1
             rounds = FIRST_USE[step] + 4 - first
             tasks = [
-                (regroup_weights, (step, 0, 0)),
-                (regroup_weights, (step, 1, 0)),
-                (regroup_weights, (step, 0, 1)),
-                (quantise_weights, (step, 0)),
-                (regroup_weights, (step, 1, 1)),
-                (quantise_weights, (step, 1)),
+                (open_weights, (step,)),
+                (regroup_minus, (step, 0)),
+                (regroup_minus, (step, 1)),
+                (regroup_plus, (step, 0)),
+                (regroup_plus, (step, 1)),
+                (quantise_minus, (step,)),
+                (regroup_box, (step, 0)),
+                (regroup_box, (step, 1)),
+                (quantise_main, (step, 0)),
+                (quantise_main, (step, 1)),
             ]
             for i, task in enumerate(tasks):
                 weight_tasks.setdefault(first + i * rounds // len(tasks), []).append(task)
@@ -433,11 +449,6 @@ def tile_classifiermodel_t_kernel(
                     first_stage(r - 2, (1,) if r - 2 >= ROUNDS - VECTOR_RELUS else ())
                 if 0 <= r - 4 < ROUNDS:
                     second_stage(r - 4)
-                for m in range(CHUNKS):
-                    if r == last_unit[m] + 3:
-                        tail_passes(m, range(STEPS - 2))
-                    if r == last_unit[m] + 4:
-                        tail_passes(m, range(STEPS - 2, STEPS))
                 if r == 0:
                     spread_out_bias()
                 if 0 <= r - roi_round - 3 < CHUNKS:

@@ -28,16 +28,16 @@ CLS_COLS = 2 * PROPOSALS
 BOX_COLS = 3 * PROPOSALS
 MAIN_COLS = 512
 OUT_COLS = BOX_COLS + CLS_COLS
-LAG = 0
-VECTOR_RELUS = 0
 SHARE = 48
-AHEAD = 6
+SPREAD = 26
+VMOD = 100
+AHEAD = 12
 
-UNITS = [
-    (t - LAG * (m == LAST), m)
-    for t in range(STEPS + LAG)
-    for m in range(CHUNKS)
-    if 0 <= t - LAG * (m == LAST) < STEPS
+UNITS = [(step, m) for step in range(STEPS - 2) for m in range(CHUNKS)] + [
+    (step, m)
+    for first in (0, CHUNKS // 2)
+    for step in (STEPS - 2, STEPS - 1)
+    for m in (first, first + 1)
 ]
 ROUNDS = len(UNITS)
 FIRST_USE = [UNITS.index((step, 0)) for step in range(STEPS)]
@@ -61,9 +61,11 @@ def tile_classifiermodel_t_kernel(
     with ExitStack() as stack:
         const = stack.enter_context(tc.tile_pool(name="const", bufs=1))
         x_pool = stack.enter_context(tc.tile_pool(name="x", bufs=AHEAD + 1))
-        raw_pool = stack.enter_context(tc.tile_pool(name="raw", bufs=3))
+        raw_pool = stack.enter_context(tc.tile_pool(name="raw", bufs=4))
         stage = stack.enter_context(tc.tile_pool(name="stage", bufs=3))
         weights = stack.enter_context(tc.tile_pool(name="weights", bufs=2))
+        codes_pool = stack.enter_context(tc.tile_pool(name="codes", bufs=3))
+        h_pool = stack.enter_context(tc.tile_pool(name="h", bufs=4))
         finish = stack.enter_context(tc.tile_pool(name="finish", bufs=2))
         planes_pool = stack.enter_context(tc.tile_pool(name="planes", bufs=CHUNKS))
         work = stack.enter_context(tc.psum_pool(name="work", bufs=4))
@@ -73,6 +75,8 @@ def tile_classifiermodel_t_kernel(
         cls_tiles = {}
         box_tiles = {}
         grouped_weights = {}
+        quantised_weights = {}
+        h_quantised = {}
         x_grouped = {}
         x_quantised = {}
         h_grouped = {}
@@ -87,12 +91,6 @@ def tile_classifiermodel_t_kernel(
         conv_scales = const.tile([P, HIDDEN], U8, align_bytes=64)
         conv_bias = const.tile([P, HALVES], F32)
         out_bias = const.tile([P, MAIN_COLS], F32)
-        h_codes = const.tile([P, STEPS, CHUNKS, HALVES, P], U32, align_bytes=64)
-        h_scales = const.tile([P, STEPS, CHUNKS, HALVES, P], U8, align_bytes=64)
-        main_codes = const.tile([P, STEPS, HALVES, MAIN_COLS], U32, align_bytes=64)
-        main_scales = const.tile([P, STEPS, HALVES, MAIN_COLS], U8, align_bytes=64)
-        minus_codes = const.tile([P, STEPS, HALVES, PROPOSALS], U32, align_bytes=64)
-        minus_scales = const.tile([P, STEPS, HALVES, PROPOSALS], U8, align_bytes=64)
         main_sums = [sums.tile([P, MAIN_COLS], F32, name="main_sum%d" % m) for m in range(CHUNKS)]
 
         def load_unit(r):
@@ -136,6 +134,11 @@ def tile_classifiermodel_t_kernel(
             w_grouped = weights.tile([P, HALVES, MAIN_COLS, PACK], BF16, align_bytes=64)
             w_minus = weights.tile([P, HALVES, PROPOSALS, PACK], BF16, align_bytes=64)
             grouped_weights[step] = (w_grouped, w_minus)
+            main_codes = codes_pool.tile([P, HALVES, MAIN_COLS], U32, align_bytes=64)
+            main_scales = codes_pool.tile([P, HALVES, MAIN_COLS], U8, align_bytes=64)
+            minus_codes = codes_pool.tile([P, HALVES, PROPOSALS], U32, align_bytes=64)
+            minus_scales = codes_pool.tile([P, HALVES, PROPOSALS], U8, align_bytes=64)
+            quantised_weights[step] = (main_codes, main_scales, minus_codes, minus_scales)
 
         def regroup_minus(step, e):
             nc.vector.tensor_scalar_mul(
@@ -161,16 +164,18 @@ def tile_classifiermodel_t_kernel(
             )
 
         def quantise_main(step, e):
+            main_codes, main_scales = quantised_weights[step][:2]
             nc.vector.quantize_mx(
-                out=main_codes[:, step, e, :].bitcast(FP8X4),
-                scales=main_scales[:, step, e, :],
+                out=main_codes[:, e, :].bitcast(FP8X4),
+                scales=main_scales[:, e, :],
                 in_=grouped_weights[step][0][:, e, :, :].rearrange("p n t -> p (n t)"),
             )
 
         def quantise_minus(step):
+            minus_codes, minus_scales = quantised_weights[step][2:]
             nc.vector.quantize_mx(
-                out=minus_codes[:, step, :, :].rearrange("p e n -> p (e n)").bitcast(FP8X4),
-                scales=minus_scales[:, step, :, :].rearrange("p e n -> p (e n)"),
+                out=minus_codes[:].rearrange("p e n -> p (e n)").bitcast(FP8X4),
+                scales=minus_scales[:].rearrange("p e n -> p (e n)"),
                 in_=grouped_weights[step][1][:].rearrange("p e n t -> p (e n t)"),
             )
 
@@ -236,23 +241,27 @@ def tile_classifiermodel_t_kernel(
             h_grouped[r] = hidden
 
         def quantise_hidden(r):
-            step, m = UNITS[r]
+            h_codes = h_pool.tile([P, HALVES, P], U32, align_bytes=64)
+            h_scales = h_pool.tile([P, HALVES, P], U8, align_bytes=64)
+            h_quantised[r] = (h_codes, h_scales)
             nc.vector.quantize_mx(
-                out=h_codes[:, step, m, :, :].rearrange("p e b -> p (e b)").bitcast(FP8X4),
-                scales=h_scales[:, step, m, :, :].rearrange("p e b -> p (e b)"),
+                out=h_codes[:].rearrange("p e b -> p (e b)").bitcast(FP8X4),
+                scales=h_scales[:].rearrange("p e b -> p (e b)"),
                 in_=h_grouped[r][:].rearrange("p e b t -> p (e b t)"),
             )
 
         def second_stage(r):
             step, m = UNITS[r]
+            h_codes, h_scales = h_quantised[r]
+            main_codes, main_scales, minus_codes, minus_scales = quantised_weights[step]
             for e in range(HALVES):
                 def main_pass():
                     nc.tensor.matmul_mx(
                         out=main_sums[m][:],
-                        lhsT=h_codes[:, step, m, e, :].bitcast(FP8X4),
-                        lhsT_scale=h_scales[:, step, m, e, :],
-                        rhs=main_codes[:, step, e, :].bitcast(FP8X4),
-                        rhs_scale=main_scales[:, step, e, :],
+                        lhsT=h_codes[:, e, :].bitcast(FP8X4),
+                        lhsT_scale=h_scales[:, e, :],
+                        rhs=main_codes[:, e, :].bitcast(FP8X4),
+                        rhs_scale=main_scales[:, e, :],
                         start=(step == 0 and e == 0),
                         stop=(step == STEPS - 1 and e == HALVES - 1),
                     )
@@ -260,10 +269,10 @@ def tile_classifiermodel_t_kernel(
                 def minus_pass():
                     nc.tensor.matmul_mx(
                         out=main_sums[m][:, BOX_COLS:],
-                        lhsT=h_codes[:, step, m, e, :].bitcast(FP8X4),
-                        lhsT_scale=h_scales[:, step, m, e, :],
-                        rhs=minus_codes[:, step, e, :].bitcast(FP8X4),
-                        rhs_scale=minus_scales[:, step, e, :],
+                        lhsT=h_codes[:, e, :].bitcast(FP8X4),
+                        lhsT_scale=h_scales[:, e, :],
+                        rhs=minus_codes[:, e, :].bitcast(FP8X4),
+                        rhs_scale=minus_scales[:, e, :],
                         start=False,
                         stop=False,
                     )
@@ -391,8 +400,6 @@ def tile_classifiermodel_t_kernel(
         weight_tasks = {}
         loads = [(r, 0, load_unit, (r,)) for r in range(ROUNDS)]
         for step in range(STEPS):
-            first = FIRST_USE[step - 1] + 4 if step else 1
-            rounds = FIRST_USE[step] + 4 - first
             tasks = [
                 (open_weights, (step,)),
                 (regroup_minus, (step, 0)),
@@ -405,14 +412,19 @@ def tile_classifiermodel_t_kernel(
                 (quantise_main, (step, 0)),
                 (quantise_main, (step, 1)),
             ]
+            first, rounds = (1, 4) if step == 0 else (5 + (step - 1) * SPREAD / (STEPS - 1), SPREAD / (STEPS - 1))
             for i, task in enumerate(tasks):
-                weight_tasks.setdefault(first + i * rounds // len(tasks), []).append(task)
-            loads.append((first, 1, load_cls, (step,)))
-            loads.append((first + 1, 1, load_box, (step, 0)))
-            loads.append((first + 2, 1, load_box, (step, 1)))
+                at = int(first + i * rounds / len(tasks))
+                weight_tasks.setdefault(at, []).append(task)
+                if i == 0:
+                    loads.append((at, 1, load_cls, (step,)))
+                elif i == 6:
+                    loads.append((at, 1, load_box, (step, 0)))
+                elif i == 7:
+                    loads.append((at, 1, load_box, (step, 1)))
         loads.sort(key=lambda load: (load[0], load[1]))
         last_unit = [UNITS.index((STEPS - 1, m)) for m in range(CHUNKS)]
-        roi_round = 12
+        roi_round = 20
 
         with tc.manual_schedule():
             nc.vector.memset(bias_row[:], 0.0)
@@ -446,7 +458,7 @@ def tile_classifiermodel_t_kernel(
                 if r < ROUNDS:
                     transpose_unit(r)
                 if 0 <= r - 2 < ROUNDS:
-                    first_stage(r - 2, (1,) if r - 2 >= ROUNDS - VECTOR_RELUS else ())
+                    first_stage(r - 2, (1,) if (r - 2) % VMOD == VMOD - 1 else ())
                 if 0 <= r - 4 < ROUNDS:
                     second_stage(r - 4)
                 if r == 0:

@@ -21,7 +21,6 @@ PROPOSALS = 128
 STRIDE = 16.0
 
 CHUNKS = BATCH // P
-LAST = CHUNKS - 1
 STEPS = POSITIONS // PACK
 HALVES = HIDDEN // P
 CLS_COLS = 2 * PROPOSALS
@@ -29,18 +28,17 @@ BOX_COLS = 3 * PROPOSALS
 MAIN_COLS = 512
 OUT_COLS = BOX_COLS + CLS_COLS
 SHARE = 48
-SPREAD = 26
-VMOD = 100
-AHEAD = 12
+AHEAD = 8
 
 UNITS = [(step, m) for step in range(STEPS - 2) for m in range(CHUNKS)] + [
-    (step, m)
-    for first in (0, CHUNKS // 2)
-    for step in (STEPS - 2, STEPS - 1)
-    for m in (first, first + 1)
+    (step, m) for m in range(CHUNKS) for step in (STEPS - 2, STEPS - 1)
 ]
 ROUNDS = len(UNITS)
-FIRST_USE = [UNITS.index((step, 0)) for step in range(STEPS)]
+FIRST_LAG = 3
+SECOND_LAG = 6
+FIRST_ROUND = [r + FIRST_LAG for r in range(ROUNDS)]
+SECOND_ROUND = [min(r + SECOND_LAG, ROUNDS + SECOND_LAG - 2) for r in range(ROUNDS)]
+WEIGHT_ROUNDS = range(3, 31)
 
 FLOPS = 2 * BATCH * POSITIONS * CHANNELS * HIDDEN + 2 * BATCH * POSITIONS * HIDDEN * OUT_COLS
 BYTES = (
@@ -62,11 +60,11 @@ def tile_classifiermodel_t_kernel(
         const = stack.enter_context(tc.tile_pool(name="const", bufs=1))
         x_pool = stack.enter_context(tc.tile_pool(name="x", bufs=AHEAD + 1))
         raw_pool = stack.enter_context(tc.tile_pool(name="raw", bufs=4))
-        stage = stack.enter_context(tc.tile_pool(name="stage", bufs=3))
+        stage = stack.enter_context(tc.tile_pool(name="stage", bufs=4))
         weights = stack.enter_context(tc.tile_pool(name="weights", bufs=2))
         codes_pool = stack.enter_context(tc.tile_pool(name="codes", bufs=3))
-        h_pool = stack.enter_context(tc.tile_pool(name="h", bufs=4))
-        finish = stack.enter_context(tc.tile_pool(name="finish", bufs=2))
+        h_pool = stack.enter_context(tc.tile_pool(name="h", bufs=6))
+        finish = stack.enter_context(tc.tile_pool(name="finish", bufs=3))
         planes_pool = stack.enter_context(tc.tile_pool(name="planes", bufs=CHUNKS))
         work = stack.enter_context(tc.psum_pool(name="work", bufs=4))
         sums = stack.enter_context(tc.psum_pool(name="sums", bufs=1))
@@ -206,7 +204,7 @@ def tile_classifiermodel_t_kernel(
             )
             x_quantised[r] = (x_codes, x_scales)
 
-        def first_stage(r, vector_halves):
+        def first_stage(r):
             x_codes, x_scales = x_quantised[r]
             hidden = stage.tile([P, HALVES, P, PACK], BF16, align_bytes=64)
             for e in range(HALVES):
@@ -221,23 +219,13 @@ def tile_classifiermodel_t_kernel(
                     stop=True,
                 )
                 h_view = h_sum[:].rearrange("p (t b) -> p b t", t=PACK)
-                if e in vector_halves:
-                    nc.vector.tensor_scalar(
-                        out=hidden[:, e, :, :],
-                        in0=h_view,
-                        scalar1=conv_bias[:, e : e + 1],
-                        scalar2=0.0,
-                        op0=ALU.add,
-                        op1=ALU.max,
-                    )
-                else:
-                    nc.scalar.activation(
-                        out=hidden[:, e, :, :],
-                        in_=h_view,
-                        func=ACT.Relu,
-                        bias=conv_bias[:, e : e + 1],
-                        scale=1.0,
-                    )
+                nc.scalar.activation(
+                    out=hidden[:, e, :, :],
+                    in_=h_view,
+                    func=ACT.Relu,
+                    bias=conv_bias[:, e : e + 1],
+                    scale=1.0,
+                )
             h_grouped[r] = hidden
 
         def quantise_hidden(r):
@@ -294,7 +282,11 @@ def tile_classifiermodel_t_kernel(
 
         def activate_sums(m):
             z = finish.tile([P, MAIN_COLS], F32)
-            nc.vector.tensor_tensor(out=z[:], in0=main_sums[m][:], in1=out_bias[:], op=ALU.add)
+            planes4 = [t[:].rearrange("p (k q) -> p k q", k=4) for t in (z, main_sums[m], out_bias)]
+            for k in (slice(1, 3), slice(0, 4, 3)):
+                nc.vector.tensor_tensor(
+                    out=planes4[0][:, k, :], in0=planes4[1][:, k, :], in1=planes4[2][:, k, :], op=ALU.add
+                )
             b23 = z[:, PROPOSALS:BOX_COLS]
             nc.vector.tensor_scalar(
                 out=b23, in0=b23, scalar1=-10.0, scalar2=10.0, op0=ALU.max, op1=ALU.min
@@ -341,26 +333,23 @@ def tile_classifiermodel_t_kernel(
                 out=result[:, 4, :], in0=halfway[:], scalar1=0.5, scalar2=0.5, op0=ALU.mult, op1=ALU.add
             )
             boxes = finish.tile([P, PROPOSALS, 5], F32)
-            scalar_share = SHARE
-            if scalar_share:
-                nc.scalar.copy(
-                    out=boxes[:, :scalar_share, :],
-                    in_=result[:, :, :scalar_share].rearrange("p k q -> p q k"),
-                )
+            nc.scalar.copy(
+                out=boxes[:, :SHARE, :], in_=result[:, :, :SHARE].rearrange("p k q -> p q k")
+            )
             nc.vector.tensor_copy(
-                out=boxes[:, scalar_share:, :],
-                in_=result[:, :, scalar_share:].rearrange("p k q -> p q k"),
+                out=boxes[:, SHARE:, :],
+                in_=result[:, :, SHARE:].rearrange("p k q -> p q k"),
             )
             nc.sync.dma_start(out=out[m * P : (m + 1) * P, :, :], in_=boxes[:])
 
         def prepare_conv():
             conv_raw = const.tile([P, PACK, HIDDEN], BF16)
-            nc.scalar.dma_start(
+            nc.sync.dma_start(
                 out=conv_raw[:].rearrange("p (u e) d -> p u (e d)", e=2),
                 in_=conv_w.rearrange("(u p e) d -> p u (e d)", p=P, e=2),
             )
             conv_bias_raw = const.tile([P, HALVES], BF16)
-            nc.scalar.dma_start(out=conv_bias_raw[:], in_=conv_b.rearrange("(p e) -> p e", e=HALVES))
+            nc.sync.dma_start(out=conv_bias_raw[:], in_=conv_b.rearrange("(p e) -> p e", e=HALVES))
             conv_grouped = const.tile([P, HALVES, P, PACK], BF16, align_bytes=64)
             nc.vector.tensor_copy(
                 out=conv_grouped[:], in_=conv_raw[:].rearrange("p t (j h) -> p h j t", h=HALVES)
@@ -373,10 +362,10 @@ def tile_classifiermodel_t_kernel(
             )
 
         def load_out_bias():
-            nc.scalar.dma_start(
+            nc.sync.dma_start(
                 out=bias_row[0:1, :BOX_COLS], in_=bbox_b[PROPOSALS:].rearrange("(a n) -> a n", a=1)
             )
-            nc.scalar.dma_start(
+            nc.sync.dma_start(
                 out=bias_row[0:1, BOX_COLS:], in_=cls_b.rearrange("(a n) -> a n", a=1)
             )
 
@@ -412,9 +401,9 @@ def tile_classifiermodel_t_kernel(
                 (quantise_main, (step, 0)),
                 (quantise_main, (step, 1)),
             ]
-            first, rounds = (1, 4) if step == 0 else (5 + (step - 1) * SPREAD / (STEPS - 1), SPREAD / (STEPS - 1))
             for i, task in enumerate(tasks):
-                at = int(first + i * rounds / len(tasks))
+                at = WEIGHT_ROUNDS[(step * len(tasks) + i) * len(WEIGHT_ROUNDS) // (STEPS * len(tasks))]
+                assert at <= SECOND_ROUND[UNITS.index((step, 0))]
                 weight_tasks.setdefault(at, []).append(task)
                 if i == 0:
                     loads.append((at, 1, load_cls, (step,)))
@@ -434,33 +423,37 @@ def tile_classifiermodel_t_kernel(
             load_out_bias()
             prepare_conv()
             issued = 1
-            for r in range(ROUNDS + 8):
+            for r in range(SECOND_ROUND[-1] + 4):
                 while issued < len(loads) and loads[issued][0] <= r + AHEAD:
                     need, rank, load, arguments = loads[issued]
                     load(*arguments)
                     issued += 1
                 if 0 <= r - roi_round < CHUNKS:
                     load_roi(r - roi_round)
-                for m in range(CHUNKS):
-                    if r == last_unit[m] + 5:
-                        activate_sums(m)
-                    if r == last_unit[m] + 6:
-                        exponentials(m)
-                    if r == last_unit[m] + 7:
-                        store_boxes(m)
-                tasks = weight_tasks.get(r, [])
-                if 0 <= r - 1 < ROUNDS:
-                    quantise_features(r - 1)
-                for task, arguments in tasks:
+                for u in range(ROUNDS):
+                    if r == FIRST_ROUND[u] - 1:
+                        quantise_features(u)
+                for task, arguments in weight_tasks.get(r, []):
                     task(*arguments)
-                if 0 <= r - 3 < ROUNDS:
-                    quantise_hidden(r - 3)
+                for u in range(ROUNDS):
+                    if r == SECOND_ROUND[u] - 1:
+                        quantise_hidden(u)
+                for m in range(CHUNKS):
+                    late = r - SECOND_ROUND[last_unit[m]]
+                    if late == 1:
+                        activate_sums(m)
+                    if late == 2:
+                        exponentials(m)
+                    if late == 3:
+                        store_boxes(m)
                 if r < ROUNDS:
                     transpose_unit(r)
-                if 0 <= r - 2 < ROUNDS:
-                    first_stage(r - 2, (1,) if (r - 2) % VMOD == VMOD - 1 else ())
-                if 0 <= r - 4 < ROUNDS:
-                    second_stage(r - 4)
+                for u in range(ROUNDS):
+                    if r == FIRST_ROUND[u]:
+                        first_stage(u)
+                for u in range(ROUNDS):
+                    if r == SECOND_ROUND[u]:
+                        second_stage(u)
                 if r == 0:
                     spread_out_bias()
                 if 0 <= r - roi_round - 3 < CHUNKS:

@@ -28,6 +28,7 @@ BOX_COLS = 3 * PROPOSALS
 MAIN_COLS = 512
 OUT_COLS = BOX_COLS + CLS_COLS
 SHARE = 48
+WARM_START, WARM_BEFORE, WARM_AFTER = 4, 2, 1
 AHEAD = 8
 
 UNITS = [(step, m) for step in range(STEPS - 2) for m in range(CHUNKS)] + [
@@ -84,6 +85,7 @@ def tile_classifiermodel_t_kernel(
 
         identity = const.tile([P, P], F32)
         ones = const.tile([P, P], BF16)
+        zeros = const.tile([P, MAIN_COLS], BF16)
         bias_row = const.tile([P, OUT_COLS], BF16)
         conv_codes = const.tile([P, HIDDEN], U32, align_bytes=64)
         conv_scales = const.tile([P, HIDDEN], U8, align_bytes=64)
@@ -176,6 +178,13 @@ def tile_classifiermodel_t_kernel(
                 scales=minus_scales[:].rearrange("p e n -> p (e n)"),
                 in_=grouped_weights[step][1][:].rearrange("p e n t -> p (e n t)"),
             )
+
+        def keep_warm(count):
+            for i in range(count):
+                nc.tensor.matmul(
+                    out=main_sums[CHUNKS - 1][:], lhsT=zeros[:, :P], rhs=zeros[:],
+                    start=True, stop=True,
+                )
 
         def transpose_unit(r):
             x_words = x_tiles[r][:].bitcast(F32)
@@ -333,12 +342,13 @@ def tile_classifiermodel_t_kernel(
                 out=result[:, 4, :], in0=halfway[:], scalar1=0.5, scalar2=0.5, op0=ALU.mult, op1=ALU.add
             )
             boxes = finish.tile([P, PROPOSALS, 5], F32)
-            nc.scalar.copy(
-                out=boxes[:, :SHARE, :], in_=result[:, :, :SHARE].rearrange("p k q -> p q k")
-            )
+            share = SHARE if m else 0
+            if share:
+                nc.scalar.copy(
+                    out=boxes[:, :share, :], in_=result[:, :, :share].rearrange("p k q -> p q k")
+                )
             nc.vector.tensor_copy(
-                out=boxes[:, SHARE:, :],
-                in_=result[:, :, SHARE:].rearrange("p k q -> p q k"),
+                out=boxes[:, share:, :], in_=result[:, :, share:].rearrange("p k q -> p q k")
             )
             nc.sync.dma_start(out=out[m * P : (m + 1) * P, :, :], in_=boxes[:])
 
@@ -416,10 +426,12 @@ def tile_classifiermodel_t_kernel(
         roi_round = 20
 
         with tc.manual_schedule():
-            nc.vector.memset(bias_row[:], 0.0)
+            nc.vector.memset(zeros[:].bitcast(U32), 0)
+            nc.vector.memset(bias_row[:].bitcast(U32), 0)
             nc.vector.memset(ones[:], 1.0)
             masks.make_identity(nc, identity[:])
             load_unit(0)
+            keep_warm(WARM_START)
             load_out_bias()
             prepare_conv()
             issued = 1
@@ -438,16 +450,14 @@ def tile_classifiermodel_t_kernel(
                 for u in range(ROUNDS):
                     if r == SECOND_ROUND[u] - 1:
                         quantise_hidden(u)
-                for m in range(CHUNKS):
-                    late = r - SECOND_ROUND[last_unit[m]]
-                    if late == 1:
-                        activate_sums(m)
-                    if late == 2:
-                        exponentials(m)
-                    if late == 3:
-                        store_boxes(m)
+                for late, part in ((1, activate_sums), (2, exponentials), (3, store_boxes)):
+                    for m in range(CHUNKS):
+                        if r == SECOND_ROUND[last_unit[m]] + late:
+                            part(m)
                 if r < ROUNDS:
                     transpose_unit(r)
+                if r < SECOND_LAG:
+                    keep_warm(WARM_BEFORE if r < FIRST_LAG else WARM_AFTER)
                 for u in range(ROUNDS):
                     if r == FIRST_ROUND[u]:
                         first_stage(u)

@@ -213,10 +213,13 @@ def tile_classifiermodel_t_kernel(
             )
             x_quantised[r] = (x_codes, x_scales)
 
-        def first_stage(r):
+        def first_stage(r, halves):
             x_codes, x_scales = x_quantised[r]
-            hidden = stage.tile([P, HALVES, P, PACK], BF16, align_bytes=64)
-            for e in range(HALVES):
+            if 0 in halves:
+                hidden = stage.tile([P, HALVES, P, PACK], BF16, align_bytes=64)
+                h_grouped[r] = hidden
+            hidden = h_grouped[r]
+            for e in halves:
                 h_sum = work.tile([P, PACK * P], F32, tag="work")
                 nc.tensor.matmul_mx(
                     out=h_sum[:],
@@ -235,7 +238,6 @@ def tile_classifiermodel_t_kernel(
                     bias=conv_bias[:, e : e + 1],
                     scale=1.0,
                 )
-            h_grouped[r] = hidden
 
         def quantise_hidden(r):
             h_codes = h_pool.tile([P, HALVES, P], U32, align_bytes=64)
@@ -247,11 +249,11 @@ def tile_classifiermodel_t_kernel(
                 in_=h_grouped[r][:].rearrange("p e b t -> p (e b t)"),
             )
 
-        def second_stage(r):
+        def second_stage(r, halves):
             step, m = UNITS[r]
             h_codes, h_scales = h_quantised[r]
             main_codes, main_scales, minus_codes, minus_scales = quantised_weights[step]
-            for e in range(HALVES):
+            for e in halves:
                 def main_pass():
                     nc.tensor.matmul_mx(
                         out=main_sums[m][:],
@@ -458,12 +460,13 @@ def tile_classifiermodel_t_kernel(
                     transpose_unit(r)
                 if r < SECOND_LAG:
                     keep_warm(WARM_BEFORE if r < FIRST_LAG else WARM_AFTER)
-                for u in range(ROUNDS):
-                    if r == FIRST_ROUND[u]:
-                        first_stage(u)
-                for u in range(ROUNDS):
-                    if r == SECOND_ROUND[u]:
-                        second_stage(u)
+                for e in range(HALVES):
+                    for u in range(ROUNDS):
+                        if r == FIRST_ROUND[u]:
+                            first_stage(u, (e,))
+                    for u in range(ROUNDS):
+                        if r == SECOND_ROUND[u]:
+                            second_stage(u, (e,))
                 if r == 0:
                     spread_out_bias()
                 if 0 <= r - roi_round - 3 < CHUNKS:

from contextlib import ExitStack

import concourse.masks as masks
import concourse.mybir as mybir

F32 = mybir.dt.float32
BF16 = mybir.dt.bfloat16
U32 = mybir.dt.uint32
U8 = mybir.dt.uint8
FP8X4 = mybir.dt.float8_e4m3fn_x4
ACT = mybir.ActivationFunctionType
ALU = mybir.AluOpType

P = 128
PACK = 4
BATCH = 512
POSITIONS = 32
CHANNELS = 512
HIDDEN = 256
PROPOSALS = 128
STRIDE = 16.0

CHUNKS = BATCH // P
STEPS = POSITIONS // PACK
HALVES = HIDDEN // P
CLS_COLS = 2 * PROPOSALS
BOX_COLS = 3 * PROPOSALS
MAIN_COLS = 512
OUT_COLS = BOX_COLS + CLS_COLS
SHARE = 48
WARM_START, WARM_BEFORE, WARM_AFTER = 4, 2, 1
AHEAD = 8

UNITS = [(step, m) for step in range(STEPS - 2) for m in range(CHUNKS)] + [
    (step, m) for m in range(CHUNKS) for step in (STEPS - 2, STEPS - 1)
]
ROUNDS = len(UNITS)
FIRST_LAG = 3
SECOND_LAG = 6
FIRST_ROUND = [r + FIRST_LAG for r in range(ROUNDS)]
SECOND_ROUND = [min(r + SECOND_LAG, ROUNDS + SECOND_LAG - 2) for r in range(ROUNDS)]
WEIGHT_ROUNDS = range(3, 31)

FLOPS = 2 * BATCH * POSITIONS * CHANNELS * HIDDEN + 2 * BATCH * POSITIONS * HIDDEN * OUT_COLS
BYTES = (
    2 * (BATCH * POSITIONS * CHANNELS + BATCH * PROPOSALS * 4 + CHANNELS * HIDDEN + HIDDEN)
    + 2 * (POSITIONS * HIDDEN + 1) * OUT_COLS
    + 4 * BATCH * PROPOSALS * 5
)


def tile_classifiermodel_t_kernel(
    tc, features, roi, conv_w, conv_b, cls_w, cls_b, bbox_w, bbox_b, out
):
    nc = tc.nc
    feature_rows = features.rearrange("b i j c -> b (i j) c")
    cls_rows = cls_w.rearrange("(s p e) n -> p s (e n)", p=P, e=HALVES)
    box_rows = bbox_w.rearrange("(s p e) n -> p s e n", p=P, e=HALVES)

    with ExitStack() as stack:
        const = stack.enter_context(tc.tile_pool(name="const", bufs=1))
        x_pool = stack.enter_context(tc.tile_pool(name="x", bufs=AHEAD + 1))
        raw_pool = stack.enter_context(tc.tile_pool(name="raw", bufs=4))
        stage = stack.enter_context(tc.tile_pool(name="stage", bufs=4))
        weights = stack.enter_context(tc.tile_pool(name="weights", bufs=2))
        codes_pool = stack.enter_context(tc.tile_pool(name="codes", bufs=3))
        h_pool = stack.enter_context(tc.tile_pool(name="h", bufs=6))
        finish = stack.enter_context(tc.tile_pool(name="finish", bufs=3))
        planes_pool = stack.enter_context(tc.tile_pool(name="planes", bufs=CHUNKS))
        work = stack.enter_context(tc.psum_pool(name="work", bufs=4))
        sums = stack.enter_context(tc.psum_pool(name="sums", bufs=1))

        x_tiles = {}
        cls_tiles = {}
        box_tiles = {}
        grouped_weights = {}
        quantised_weights = {}
        h_quantised = {}
        x_grouped = {}
        x_quantised = {}
        h_grouped = {}
        roi_tiles = {}
        planes = {}
        activated = {}

        identity = const.tile([P, P], F32)
        ones = const.tile([P, P], BF16)
        zeros = const.tile([P, MAIN_COLS], BF16)
        bias_row = const.tile([P, OUT_COLS], BF16)
        conv_codes = const.tile([P, HIDDEN], U32, align_bytes=64)
        conv_scales = const.tile([P, HIDDEN], U8, align_bytes=64)
        conv_bias = const.tile([P, HALVES], F32)
        out_bias = const.tile([P, MAIN_COLS], F32)
        main_sums = [sums.tile([P, MAIN_COLS], F32, name="main_sum%d" % m) for m in range(CHUNKS)]

        def load_unit(r):
            step, m = UNITS[r]
            x = x_pool.tile([P, PACK, CHANNELS], BF16)
            pieces = 2 if r == 0 else 1
            width = PACK // pieces
            for piece in range(pieces):
                first = step * PACK + piece * width
                nc.sync.dma_start(
                    out=x[:, piece * width : (piece + 1) * width, :],
                    in_=feature_rows[m * P : (m + 1) * P, first : first + width, :],
                )
            x_tiles[r] = x

        def load_cls(step):
            cls_raw = raw_pool.tile([P, PACK, HALVES, CLS_COLS], BF16)
            nc.sync.dma_start(
                out=cls_raw[:].rearrange("p t e n -> p t (e n)"),
                in_=cls_rows[:, step * PACK : (step + 1) * PACK, :],
            )
            cls_tiles[step] = cls_raw

        def load_box(step, e):
            if e == 0:
                box_raw = raw_pool.tile([P, PACK, HALVES, BOX_COLS], BF16)
                box_tiles[step] = box_raw
            nc.sync.dma_start(
                out=box_tiles[step][:, :, e, :],
                in_=box_rows[:, step * PACK : (step + 1) * PACK, e, PROPOSALS:],
            )

        def load_roi(m):
            roi_raw = planes_pool.tile([P, PROPOSALS * 4], BF16)
            nc.sync.dma_start(
                out=roi_raw[:], in_=roi[m * P : (m + 1) * P, :, :].rearrange("b q k -> b (q k)")
            )
            roi_tiles[m] = roi_raw

        def open_weights(step):
            w_grouped = weights.tile([P, HALVES, MAIN_COLS, PACK], BF16, align_bytes=64)
            w_minus = weights.tile([P, HALVES, PROPOSALS, PACK], BF16, align_bytes=64)
            grouped_weights[step] = (w_grouped, w_minus)
            main_codes = codes_pool.tile([P, HALVES, MAIN_COLS], U32, align_bytes=64)
            main_scales = codes_pool.tile([P, HALVES, MAIN_COLS], U8, align_bytes=64)
            minus_codes = codes_pool.tile([P, HALVES, PROPOSALS], U32, align_bytes=64)
            minus_scales = codes_pool.tile([P, HALVES, PROPOSALS], U8, align_bytes=64)
            quantised_weights[step] = (main_codes, main_scales, minus_codes, minus_scales)

        def regroup_minus(step, e):
            nc.vector.tensor_scalar_mul(
                out=grouped_weights[step][1][:, e, :, :].rearrange("p (c i) t -> p c t i", i=4),
                in0=cls_tiles[step][:, :, e, :PROPOSALS].rearrange("p t (c i) -> p c t i", i=4),
                scalar1=-1.0,
            )

        def regroup_plus(step, e):
            nc.vector.tensor_copy(
                out=grouped_weights[step][0][:, e, BOX_COLS:, :].rearrange(
                    "p (c i) t -> p c t i", i=4
                ),
                in_=cls_tiles[step][:, :, e, PROPOSALS:].rearrange("p t (c i) -> p c t i", i=4),
            )

        def regroup_box(step, e):
            nc.vector.tensor_copy(
                out=grouped_weights[step][0][:, e, :BOX_COLS, :].rearrange(
                    "p (c i) t -> p c t i", i=4
                ),
                in_=box_tiles[step][:, :, e, :].rearrange("p t (c i) -> p c t i", i=4),
            )

        def quantise_main(step, e):
            main_codes, main_scales = quantised_weights[step][:2]
            nc.vector.quantize_mx(
                out=main_codes[:, e, :].bitcast(FP8X4),
                scales=main_scales[:, e, :],
                in_=grouped_weights[step][0][:, e, :, :].rearrange("p n t -> p (n t)"),
            )

        def quantise_minus(step):
            minus_codes, minus_scales = quantised_weights[step][2:]
            nc.vector.quantize_mx(
                out=minus_codes[:].rearrange("p e n -> p (e n)").bitcast(FP8X4),
                scales=minus_scales[:].rearrange("p e n -> p (e n)"),
                in_=grouped_weights[step][1][:].rearrange("p e n t -> p (e n t)"),
            )

        def keep_warm(count):
            for i in range(count):
                nc.tensor.matmul(
                    out=main_sums[CHUNKS - 1][:], lhsT=zeros[:, :P], rhs=zeros[:],
                    start=True, stop=True,
                )

        def transpose_unit(r):
            x_words = x_tiles[r][:].bitcast(F32)
            grouped = stage.tile([P, PACK * P * PACK], BF16, align_bytes=64)
            grouped_words = grouped[:].bitcast(F32).rearrange("p (r u) -> p r u", u=2)
            for bank in range(2):
                turned = work.tile([P, 2, 2 * P], F32, tag="work")
                for tt in range(2):
                    for u in range(2):
                        nc.tensor.transpose(
                            turned[:, u, tt * P : (tt + 1) * P],
                            x_words[:, 2 * bank + tt, u * P : (u + 1) * P],
                            identity[:],
                        )
                nc.scalar.copy(
                    out=grouped_words[:, bank * 2 * P : (bank + 1) * 2 * P, :],
                    in_=turned[:].rearrange("p u r -> p r u"),
                )
            x_grouped[r] = grouped

        def quantise_features(r):
            x_codes = stage.tile([P, PACK * P], U32, align_bytes=64)
            x_scales = stage.tile([P, PACK * P], U8, align_bytes=64)
            nc.vector.quantize_mx(
                out=x_codes[:].bitcast(FP8X4), scales=x_scales[:], in_=x_grouped[r][:]
            )
            x_quantised[r] = (x_codes, x_scales)

        def first_stage(r, halves):
            x_codes, x_scales = x_quantised[r]
            if 0 in halves:
                hidden = stage.tile([P, HALVES, P, PACK], BF16, align_bytes=64)
                h_grouped[r] = hidden
            hidden = h_grouped[r]
            for e in halves:
                h_sum = work.tile([P, PACK * P], F32, tag="work")
                nc.tensor.matmul_mx(
                    out=h_sum[:],
                    lhsT=conv_codes[:, e * P : (e + 1) * P].bitcast(FP8X4),
                    lhsT_scale=conv_scales[:, e * P : (e + 1) * P],
                    rhs=x_codes[:].bitcast(FP8X4),
                    rhs_scale=x_scales[:],
                    start=True,
                    stop=True,
                )
                h_view = h_sum[:].rearrange("p (t b) -> p b t", t=PACK)
                nc.scalar.activation(
                    out=hidden[:, e, :, :],
                    in_=h_view,
                    func=ACT.Relu,
                    bias=conv_bias[:, e : e + 1],
                    scale=1.0,
                )

        def quantise_hidden(r):
            h_codes = h_pool.tile([P, HALVES, P], U32, align_bytes=64)
            h_scales = h_pool.tile([P, HALVES, P], U8, align_bytes=64)
            h_quantised[r] = (h_codes, h_scales)
            nc.vector.quantize_mx(
                out=h_codes[:].rearrange("p e b -> p (e b)").bitcast(FP8X4),
                scales=h_scales[:].rearrange("p e b -> p (e b)"),
                in_=h_grouped[r][:].rearrange("p e b t -> p (e b t)"),
            )

        def second_stage(r, halves):
            step, m = UNITS[r]
            h_codes, h_scales = h_quantised[r]
            main_codes, main_scales, minus_codes, minus_scales = quantised_weights[step]
            for e in halves:
                def main_pass():
                    nc.tensor.matmul_mx(
                        out=main_sums[m][:],
                        lhsT=h_codes[:, e, :].bitcast(FP8X4),
                        lhsT_scale=h_scales[:, e, :],
                        rhs=main_codes[:, e, :].bitcast(FP8X4),
                        rhs_scale=main_scales[:, e, :],
                        start=(step == 0 and e == 0),
                        stop=(step == STEPS - 1 and e == HALVES - 1),
                    )

                def minus_pass():
                    nc.tensor.matmul_mx(
                        out=main_sums[m][:, BOX_COLS:],
                        lhsT=h_codes[:, e, :].bitcast(FP8X4),
                        lhsT_scale=h_scales[:, e, :],
                        rhs=minus_codes[:, e, :].bitcast(FP8X4),
                        rhs_scale=minus_scales[:, e, :],
                        start=False,
                        stop=False,
                    )

                for one_pass in (main_pass, minus_pass) if e == 0 else (minus_pass, main_pass):
                    one_pass()

        def copy_y(m):
            result = planes_pool.tile([P, 5, PROPOSALS], F32)
            planes[m] = result
            nc.gpsimd.tensor_scalar(
                out=result[:, 1, :],
                in0=roi_tiles[m][:].rearrange("p (q k) -> p k q", k=4)[:, 1, :],
                scalar1=STRIDE,
                scalar2=0.0,
                op0=ALU.mult,
                op1=ALU.add,
            )

        def activate_sums(m):
            z = finish.tile([P, MAIN_COLS], F32)
            planes4 = [t[:].rearrange("p (k q) -> p k q", k=4) for t in (z, main_sums[m], out_bias)]
            for k in (slice(1, 3), slice(0, 4, 3)):
                nc.vector.tensor_tensor(
                    out=planes4[0][:, k, :], in0=planes4[1][:, k, :], in1=planes4[2][:, k, :], op=ALU.add
                )
            b23 = z[:, PROPOSALS:BOX_COLS]
            nc.vector.tensor_scalar(
                out=b23, in0=b23, scalar1=-10.0, scalar2=10.0, op0=ALU.max, op1=ALU.min
            )
            activated[m] = z

        def exponentials(m):
            result = planes[m]
            roi_planes = roi_tiles[m][:].rearrange("p (q k) -> p k q", k=4)
            z = activated[m]
            logit = z[:, BOX_COLS:]
            b1 = z[:, :PROPOSALS]
            b23 = z[:, PROPOSALS:BOX_COLS]
            growth = finish.tile([P, 2, PROPOSALS], F32)
            nc.scalar.activation(
                out=growth[:].rearrange("p j q -> p (j q)"), in_=b23, func=ACT.Exp
            )
            halfway = finish.tile([P, PROPOSALS], F32)
            nc.scalar.activation(out=halfway[:], in_=logit, func=ACT.Tanh, scale=0.5)
            shift = finish.tile([P, PROPOSALS], F32)
            nc.gpsimd.tensor_tensor(out=shift[:], in0=b1, in1=roi_planes[:, 3, :], op=ALU.mult)
            nc.gpsimd.tensor_tensor(
                out=shift[:], in0=roi_planes[:, 0, :], in1=shift[:], op=ALU.subtract
            )
            nc.gpsimd.tensor_scalar(
                out=result[:, 0, :], in0=shift[:], scalar1=STRIDE, scalar2=0.0,
                op0=ALU.mult, op1=ALU.add,
            )
            activated[m] = (halfway, growth)

        def store_boxes(m):
            result = planes[m]
            roi_planes = roi_tiles[m][:].rearrange("p (q k) -> p k q", k=4)
            halfway, growth = activated[m]
            nc.vector.scalar_tensor_tensor(
                out=result[:, 2:4, :],
                in0=roi_planes[:, 2:4, :],
                scalar=STRIDE,
                in1=growth[:],
                op0=ALU.mult,
                op1=ALU.mult,
            )
            nc.vector.tensor_scalar(
                out=result[:, 4, :], in0=halfway[:], scalar1=0.5, scalar2=0.5, op0=ALU.mult, op1=ALU.add
            )
            boxes = finish.tile([P, PROPOSALS, 5], F32)
            share = SHARE if m else 0
            if share:
                nc.scalar.copy(
                    out=boxes[:, :share, :], in_=result[:, :, :share].rearrange("p k q -> p q k")
                )
            nc.vector.tensor_copy(
                out=boxes[:, share:, :], in_=result[:, :, share:].rearrange("p k q -> p q k")
            )
            nc.sync.dma_start(out=out[m * P : (m + 1) * P, :, :], in_=boxes[:])

        def prepare_conv():
            conv_raw = const.tile([P, PACK, HIDDEN], BF16)
            nc.sync.dma_start(
                out=conv_raw[:].rearrange("p (u e) d -> p u (e d)", e=2),
                in_=conv_w.rearrange("(u p e) d -> p u (e d)", p=P, e=2),
            )
            conv_bias_raw = const.tile([P, HALVES], BF16)
            nc.sync.dma_start(out=conv_bias_raw[:], in_=conv_b.rearrange("(p e) -> p e", e=HALVES))
            conv_grouped = const.tile([P, HALVES, P, PACK], BF16, align_bytes=64)
            nc.vector.tensor_copy(
                out=conv_grouped[:], in_=conv_raw[:].rearrange("p t (j h) -> p h j t", h=HALVES)
            )
            nc.vector.tensor_copy(out=conv_bias[:], in_=conv_bias_raw[:])
            nc.vector.quantize_mx(
                out=conv_codes[:].bitcast(FP8X4),
                scales=conv_scales[:],
                in_=conv_grouped[:].rearrange("p h j t -> p (h j t)"),
            )

        def load_out_bias():
            nc.sync.dma_start(
                out=bias_row[0:1, :BOX_COLS], in_=bbox_b[PROPOSALS:].rearrange("(a n) -> a n", a=1)
            )
            nc.sync.dma_start(
                out=bias_row[0:1, BOX_COLS:], in_=cls_b.rearrange("(a n) -> a n", a=1)
            )

        def spread_out_bias():
            for i, columns in enumerate((slice(BOX_COLS, OUT_COLS), slice(0, BOX_COLS))):
                spread = work.tile([P, columns.stop - columns.start], F32, tag="work")
                nc.tensor.matmul(
                    out=spread[:], lhsT=ones[:], rhs=bias_row[:, columns], start=True, stop=True
                )
                if i:
                    nc.scalar.copy(out=out_bias[:, :BOX_COLS], in_=spread[:])
                else:
                    cls_bias = const.tile([P, CLS_COLS], F32)
                    nc.scalar.copy(out=cls_bias[:], in_=spread[:])
                    nc.vector.tensor_sub(
                        out=out_bias[:, BOX_COLS:],
                        in0=cls_bias[:, PROPOSALS:],
                        in1=cls_bias[:, :PROPOSALS],
                    )

        weight_tasks = {}
        loads = [(r, 0, load_unit, (r,)) for r in range(ROUNDS)]
        for step in range(STEPS):
            tasks = [
                (open_weights, (step,)),
                (regroup_minus, (step, 0)),
                (regroup_minus, (step, 1)),
                (regroup_plus, (step, 0)),
                (regroup_plus, (step, 1)),
                (quantise_minus, (step,)),
                (regroup_box, (step, 0)),
                (regroup_box, (step, 1)),
                (quantise_main, (step, 0)),
                (quantise_main, (step, 1)),
            ]
            for i, task in enumerate(tasks):
                at = WEIGHT_ROUNDS[(step * len(tasks) + i) * len(WEIGHT_ROUNDS) // (STEPS * len(tasks))]
                assert at <= SECOND_ROUND[UNITS.index((step, 0))]
                weight_tasks.setdefault(at, []).append(task)
                if i == 0:
                    loads.append((at, 1, load_cls, (step,)))
                elif i == 6:
                    loads.append((at, 1, load_box, (step, 0)))
                elif i == 7:
                    loads.append((at, 1, load_box, (step, 1)))
        loads.sort(key=lambda load: (load[0], load[1]))
        last_unit = [UNITS.index((STEPS - 1, m)) for m in range(CHUNKS)]
        roi_round = 20

        with tc.manual_schedule():
            nc.vector.memset(zeros[:].bitcast(U32), 0)
            nc.vector.memset(bias_row[:].bitcast(U32), 0)
            nc.vector.memset(ones[:], 1.0)
            masks.make_identity(nc, identity[:])
            load_unit(0)
            keep_warm(WARM_START)
            load_out_bias()
            prepare_conv()
            issued = 1
            for r in range(SECOND_ROUND[-1] + 4):
                while issued < len(loads) and loads[issued][0] <= r + AHEAD:
                    need, rank, load, arguments = loads[issued]
                    load(*arguments)
                    issued += 1
                if 0 <= r - roi_round < CHUNKS:
                    load_roi(r - roi_round)
                for u in range(ROUNDS):
                    if r == FIRST_ROUND[u] - 1:
                        quantise_features(u)
                for task, arguments in weight_tasks.get(r, []):
                    task(*arguments)
                for u in range(ROUNDS):
                    if r == SECOND_ROUND[u] - 1:
                        quantise_hidden(u)
                for late, part in ((1, activate_sums), (2, exponentials), (3, store_boxes)):
                    for m in range(CHUNKS):
                        if r == SECOND_ROUND[last_unit[m]] + late:
                            part(m)
                if r < ROUNDS:
                    transpose_unit(r)
                if r < SECOND_LAG:
                    keep_warm(WARM_BEFORE if r < FIRST_LAG else WARM_AFTER)
                for e in range(HALVES):
                    for u in range(ROUNDS):
                        if r == FIRST_ROUND[u]:
                            first_stage(u, (e,))
                    for u in range(ROUNDS):
                        if r == SECOND_ROUND[u]:
                            second_stage(u, (e,))
                if r == 0:
                    spread_out_bias()
                if 0 <= r - roi_round - 3 < CHUNKS:
                    copy_y(r - roi_round - 3)
